import numpy as np
import ml_dtypes


def mxq(x, axis, fmt="e4m3"):
    dtype, down = {"e4m3": (ml_dtypes.float8_e4m3fn, 7), "e5m2": (ml_dtypes.float8_e5m2, 14)}[fmt]
    v = np.moveaxis(np.asarray(x, np.float32).astype(ml_dtypes.bfloat16).astype(np.float64), axis, -1)
    blocks = v.reshape(v.shape[:-1] + (-1, 32))
    amax = np.abs(blocks).max(-1, keepdims=True)
    byte = np.maximum(np.where(amax > 0, np.frexp(amax)[1] - 1 + 127, 0) - down, 1)
    scale = np.exp2(byte - 127.0)
    codes = (blocks / scale).astype(np.float32).astype(dtype).astype(np.float64)
    return np.moveaxis((codes * scale).reshape(v.shape), -1, axis)


WIDE = False


def mx_kscale(k):
    if not WIDE:
        return np.ones(k)
    levels = np.array([10, -10, 5, -5, 0])
    if k % 512:
        return np.exp2(np.random.permutation(np.resize(levels, k // 32))).repeat(32)
    a = np.empty((k // 512, 16))
    for p in range(k // 512):
        a[p, :8] = np.random.permutation(np.resize(levels, 8))
        for g in range(8):
            far = levels[np.abs(levels - a[p, g]) >= 10]
            a[p, g + 8] = far[np.random.randint(len(far))]
    return np.exp2(a.ravel()).repeat(32)


BF16 = ml_dtypes.bfloat16


def bf(x):
    return np.asarray(x, np.float32).astype(BF16)


def f64(x):
    return np.asarray(x).astype(np.float64)


N, D, H, E = 1024, 512, 2048, 8

CLAMP_MAX = float(np.log(100.0))


def draw0():
    s, t = mx_kscale(D), mx_kscale(H)
    return {"x": bf(np.random.standard_normal((N, D)) * s),
            "W1": bf(np.random.standard_normal((E, D, H)) / np.sqrt(D) / s[:, None] * t),
            "b1": bf(np.random.standard_normal((E, H)) * 0.1 * t),
            "W2": bf(np.random.standard_normal((E, H, D)) / np.sqrt(H) / t[:, None]),
            "b2": bf(np.random.standard_normal((E, D)) * 0.1),
            "temperature": bf(np.log(2.0) + 0.1 * np.random.standard_normal((1,)))}


def core(x, W1, b1, W2, b2, temperature):
    xe = f64(x).reshape(E, N // E, D)
    h = np.maximum((mxq(xe, 2, "e4m3") @ mxq(f64(W1), 1, "e4m3")) + f64(b1)[:, None, :], 0.0)
    y = (mxq(h, 2, "e4m3") @ mxq(f64(W2), 1, "e4m3")) + f64(b2)[:, None, :]
    logit_scale = np.exp(np.minimum(f64(temperature), CLAMP_MAX))
    return y.reshape(N, D) * logit_scale


def e4m3fn_bytes(y):
    return np.clip(np.asarray(y, np.float64), -448.0, 448.0).astype(np.float32).astype(ml_dtypes.float8_e4m3fn).view(np.uint8)


def e4m3fn_values(b):
    return np.asarray(b, np.uint8).view(ml_dtypes.float8_e4m3fn).astype(np.float64)


def setup_inputs():
    d = draw0()
    x0 = np.asarray(d['W2']).astype(np.float64)
    s = (np.max(np.abs(x0), axis=(0, 2), keepdims=True) / 448.0).astype(np.float32)
    out = {}
    for k, v in d.items():
        if k == 'W2':
            out['W2_bytes'] = e4m3fn_bytes(x0 / s.astype(np.float64))
            out['W2_scale'] = s
        else:
            out[k] = v
    return out


def reference(x, W1, b1, W2_bytes, W2_scale, b2, temperature):
    return core(x, W1, b1, e4m3fn_values(W2_bytes) * W2_scale.astype(np.float64), b2, temperature)

@@ -1,0 +1,314 @@
+import math
+from contextlib import ExitStack
+
+import concourse.mybir as mybir
+from concourse.masks import make_identity
+
+F32 = mybir.dt.float32
+BF16 = mybir.dt.bfloat16
+U32 = mybir.dt.uint32
+U8 = mybir.dt.uint8
+FP8 = mybir.dt.float8_e4m3fn
+FP8X4 = mybir.dt.float8_e4m3fn_x4
+ALU = mybir.AluOpType
+ACT = mybir.ActivationFunctionType
+
+N, D, H, E = 1024, 512, 2048, 8
+P = 128
+TOK = N // E
+G = H // 512
+DRING = 8
+Q_LAG = 2
+W_LAG = 2
+RELU_LAG = 3
+D_ENG = "sssv"
+H_SPLIT = 0
+CLAMP_MAX = float(math.log(100.0))
+FLOPS = 2 * N * D * H * 2
+
+
+def tile_moelayer_kernel(tc, x, W1, b1, W2_bytes, W2_scale, b2, temperature, out):
+    nc = tc.nc
+
+    def split_copy(dst, src, s_part):
+        if s_part > 0:
+            nc.scalar.copy(out=dst[:, 0:s_part], in_=src[:, 0:s_part])
+        if s_part < dst.shape[1]:
+            nc.vector.tensor_copy(out=dst[:, s_part:dst.shape[1]], in_=src[:, s_part:dst.shape[1]])
+
+    def copy(engine, dst, src):
+        if engine == "v":
+            nc.vector.tensor_copy(out=dst, in_=src)
+        else:
+            nc.scalar.copy(out=dst, in_=src)
+
+    with ExitStack() as ctx:
+        ctx.enter_context(tc.manual_schedule())
+        const = ctx.enter_context(tc.tile_pool(name="const", bufs=1))
+        raw_pool = ctx.enter_context(tc.tile_pool(name="raw_pool", bufs=2))
+        byte_pool = ctx.enter_context(tc.tile_pool(name="byte_pool", bufs=6))
+        work = ctx.enter_context(tc.tile_pool(name="work", bufs=3))
+        grp_pool = ctx.enter_context(tc.tile_pool(name="grp_pool", bufs=4))
+        w2_codes = ctx.enter_context(tc.tile_pool(name="w2_codes", bufs=10))
+        hq_pool = ctx.enter_context(tc.tile_pool(name="hq_pool", bufs=3))
+        out_pool = ctx.enter_context(tc.tile_pool(name="out_pool", bufs=2))
+        ps_t = ctx.enter_context(tc.psum_pool(name="ps_t", bufs=2))
+        ps_h = ctx.enter_context(tc.psum_pool(name="ps_h", bufs=4))
+        ps_y = ctx.enter_context(tc.psum_pool(name="ps_y", bufs=2))
+
+        w1_raw, w2_raw, b2_tile, turned = {}, {}, {}, {}
+
+        def load_direct(e, g):
+            raw = raw_pool.tile([P, 4, 512], BF16, name="raw_d", align_bytes=64, bufs=DRING)
+            nc.sync.dma_start(
+                out=raw[:], in_=W1[e].rearrange("(p j) n -> p j n", j=4)[:, :, g * 512:(g + 1) * 512]
+            )
+            w1_raw[e, g] = raw
+
+        def load_w2(e, half):
+            wb = byte_pool.tile([P, 2, 2048], U8, name="wb", align_bytes=64)
+            src = W2_bytes[e].rearrange("(g p s) n -> p g (s n)", p=P, s=4)[:, 2 * half:2 * half + 2, :]
+            if e == 0 and half == 0:
+                for g in range(2):
+                    nc.sync.dma_start(out=wb[:, g, :], in_=src[:, g, :])
+            else:
+                nc.sync.dma_start(out=wb[:], in_=src)
+            w2_raw[e, half] = wb
+
+        rows = out_pool.tile([P, 512], F32, name="rows", tag="y", align_bytes=64)
+        nc.vector.memset(rows[:], 0.0)
+        nc.sync.dma_start(out=rows[32:36, :], in_=W2_scale.rearrange("o (g c) z -> (o g) (c z)", c=512))
+        b1_rows = out_pool.tile([32, 512], BF16, name="b1_rows", tag="b2_row", align_bytes=64, bufs=4)
+        nc.sync.dma_start(out=b1_rows[:], in_=b1.rearrange("e (g c) -> (e g) c", c=512))
+        load_direct(0, 0)
+        load_w2(0, 0)
+        load_w2(0, 1)
+        x_all = const.tile([P, E, D], BF16, name="x_all", align_bytes=64)
+        x_src = x.rearrange("(e p) d -> p e d", p=P)
+        nc.sync.dma_start(out=x_all[:, 0:2, :], in_=x_src[:, 0:2, :])
+        temp = const.tile([P, 1], BF16, name="temp", align_bytes=64)
+        nc.sync.dma_start(out=temp[:], in_=temperature.partition_broadcast(P))
+        for g in range(1, G):
+            load_direct(0, g)
+        load_w2(1, 0)
+        load_direct(1, 0)
+
+        ident = const.tile([P, P], F32, name="ident", align_bytes=64)
+        make_identity(nc, ident[:])
+
+        nc.vector.tensor_copy(out=rows[0:32, :], in_=b1_rows[:])
+        rows_s = out_pool.tile([P, 4, P], F32, name="rows_s", tag="bg", align_bytes=64)
+        nc.vector.tensor_copy(out=rows_s[:], in_=rows[:].rearrange("r (m s) -> r s m", s=4))
+        col_ps = ps_t.tile([P, 4, P], F32, name="tp")
+        for s in range(4):
+            nc.tensor.transpose(col_ps[:, s, :], rows_s[:, s, :], ident[:])
+        cols = const.tile([P, 36, 4], F32, name="cols", align_bytes=64)
+        nc.vector.tensor_copy(out=cols[:], in_=col_ps[:, :, 0:36].rearrange("p s r -> p r s"))
+
+        xq = const.tile([P, E, TOK], U32, name="xq", align_bytes=64)
+        xs = const.tile([P, E, TOK], U8, name="xs", align_bytes=64)
+        xg_t, gain = {}, const.tile([P, 1], F32, name="gain", align_bytes=64)
+
+        def gain_calc():
+            clamped = const.tile([P, 1], F32, name="clamped", align_bytes=64)
+            nc.vector.tensor_scalar_min(clamped[:], temp[:], CLAMP_MAX)
+            nc.scalar.activation(out=gain[:], in_=clamped[:], func=ACT.Exp)
+
+        def x_turn(k):
+            tp = ps_t.tile([P, 4, P], F32, name="tp")
+            for i in range(2):
+                words = x_all[:, 2 * k + i, :].bitcast(F32)
+                for u in range(2):
+                    nc.tensor.transpose(tp[:, 2 * i + u, :], words[:, u:256:2], ident[:])
+            xg = work.tile([P, 2, TOK, 4], BF16, name="xg", align_bytes=64, bufs=1)
+            for i in range(2):
+                copy("s", xg[:, i, :, :].bitcast(F32), tp[:, 2 * i:2 * i + 2, :].rearrange("p u r -> p r u"))
+            xg_t[k] = xg
+
+        def x_quantise(k):
+            nc.vector.quantize_mx(
+                out=xq[:, 2 * k:2 * k + 2, :].rearrange("p e r -> p (e r)").bitcast(FP8X4),
+                scales=xs[:, 2 * k:2 * k + 2, :].rearrange("p e r -> p (e r)"),
+                in_=xg_t[k][:].rearrange("p e r t -> p (e r t)"),
+            )
+
+        w1_grp, w1_cod, w2_pl, w2_grp, w2_cod, h_ps, h_pl, h_grp, h_cod, y_ps, b2g = ({} for i in range(11))
+
+        def direct_interleave(e, g):
+            grp = grp_pool.tile([P, 4, P, 4], BF16, name="w1g", align_bytes=64)
+            src = w1_raw[e, g][:].rearrange("p j (m s) -> p m s j", s=4)
+            dst = grp[:].rearrange("p s m j -> p m s j")
+            if D_ENG[(G * e + g) % len(D_ENG)] == "v":
+                nc.vector.tensor_copy(out=dst, in_=src)
+            else:
+                nc.scalar.copy(out=dst, in_=src)
+            w1_grp[e, g] = grp
+
+        def direct_quantise(e, g):
+            q = grp_pool.tile([P, 512], U32, name="w1q", align_bytes=64)
+            sc = grp_pool.tile([P, 512], U8, name="w1s", align_bytes=64)
+            nc.vector.quantize_mx(
+                out=q[:].bitcast(FP8X4), scales=sc[:],
+                in_=w1_grp[e, g][:].rearrange("p s m j -> p (s m j)"),
+            )
+            w1_cod[e, g] = (q, sc)
+
+        def direct_mm1(e, g):
+            q, sc = w1_cod[e, g]
+            ph = ps_h.tile([P, 4, TOK], F32, name="ph")
+            for s in range(4):
+                nc.tensor.matmul_mx(
+                    out=ph[:, s, :],
+                    lhsT=q[:, s * P:(s + 1) * P].bitcast(FP8X4), lhsT_scale=sc[:, s * P:(s + 1) * P],
+                    rhs=xq[:, e, :].bitcast(FP8X4), rhs_scale=xs[:, e, :],
+                    start=True, stop=True,
+                )
+            for s in range(4):
+                h_ps[e, g, s] = ph[:, s, :]
+
+        def h_relu(e, g, s):
+            if e not in h_pl:
+                h_pl[e] = work.tile([P, 4, G * TOK], BF16, name="hp", align_bytes=64, bufs=4)
+            nc.scalar.activation(
+                out=h_pl[e][:, s, g * TOK:(g + 1) * TOK], in_=h_ps[e, g, s],
+                func=ACT.Relu, bias=cols[:, 4 * e + g, s:s + 1],
+            )
+
+        def h_interleave(e):
+            grp = work.tile([P, G * TOK, 4], BF16, name="hg", align_bytes=64, bufs=2)
+            split_copy(
+                grp[:].rearrange("p (c i) s -> p c s i", i=4),
+                h_pl[e][:].rearrange("p s (c i) -> p c s i", i=4),
+                64 if e >= 6 else H_SPLIT,
+            )
+            h_grp[e] = grp
+
+        def h_quantise(e):
+            q = hq_pool.tile([P, G * TOK], U32, name="hq", align_bytes=64)
+            sc = hq_pool.tile([P, G * TOK], U8, name="hs", align_bytes=64)
+            nc.vector.quantize_mx(
+                out=q[:].bitcast(FP8X4), scales=sc[:], in_=h_grp[e][:].rearrange("p n s -> p (n s)")
+            )
+            h_cod[e] = (q, sc)
+
+        def w2_widen(e, g):
+            plane = work.tile([P, 2, 512, 2], BF16, name="w2p", align_bytes=64, bufs=3)
+            for s in (0, 2, 1, 3):
+                nc.vector.tensor_scalar(
+                    out=plane[:, s // 2, :, s % 2],
+                    in0=w2_raw[e, g // 2][:, g % 2, s * 512:(s + 1) * 512].bitcast(FP8),
+                    scalar1=cols[:, 32 + g, s:s + 1], scalar2=None, op0=ALU.mult,
+                )
+            w2_pl[e, g] = plane
+
+        def w2_interleave(e, g):
+            grp = work.tile([P, 512, 4], BF16, name="w2g", align_bytes=64, bufs=4)
+            nc.scalar.copy(
+                out=grp[:].bitcast(F32),
+                in_=w2_pl[e, g][:].rearrange("p h n l -> p h (n l)").bitcast(F32).rearrange("p h n -> p n h"),
+            )
+            w2_grp[e, g] = grp
+
+        def w2_quantise(e, g):
+            q = w2_codes.tile([P, 512], U32, name="w2q", align_bytes=64)
+            sc = w2_codes.tile([P, 512], U8, name="w2s", align_bytes=64)
+            nc.vector.quantize_mx(
+                out=q[:].bitcast(FP8X4), scales=sc[:], in_=w2_grp[e, g][:].rearrange("p n s -> p (n s)")
+            )
+            w2_cod[e, g] = (q, sc)
+
+        def mm2(e):
+            py = ps_y.tile([TOK, D], F32, name="py")
+            hq, hs = h_cod[e]
+            for g in range(G):
+                wq, ws = w2_cod[e, g]
+                c = slice(g * TOK, (g + 1) * TOK)
+                nc.tensor.matmul_mx(
+                    out=py[:], lhsT=hq[:, c].bitcast(FP8X4), lhsT_scale=hs[:, c],
+                    rhs=wq[:].bitcast(FP8X4), rhs_scale=ws[:],
+                    start=(g == 0), stop=(g == G - 1),
+                )
+            y_ps[e] = py
+
+        def b2_load(experts):
+            for e in experts:
+                b2_tile[e] = out_pool.tile([P, D], BF16, name="b2_row", align_bytes=64, bufs=4)
+                nc.sync.dma_start(out=b2_tile[e][:], in_=b2[e, :].partition_broadcast(P))
+
+        def bias2(e):
+            bg = out_pool.tile([P, D], F32, name="bg", align_bytes=64)
+            nc.vector.tensor_scalar(
+                out=bg[:], in0=b2_tile[e][:], scalar1=gain[:], scalar2=None, op0=ALU.mult
+            )
+            b2g[e] = bg
+
+        def store(e):
+            y = out_pool.tile([TOK, D], F32, name="y", align_bytes=64)
+            nc.vector.scalar_tensor_tensor(
+                out=y[:], in0=y_ps[e][:], scalar=gain[:], in1=b2g[e][:], op0=ALU.mult, op1=ALU.add
+            )
+            nc.sync.dma_start(out=out[e * TOK:(e + 1) * TOK, :], in_=y[:])
+
+        h_jobs = {}
+
+        def finish(n, experts):
+            for j, e in enumerate(experts):
+                h_jobs.setdefault(n + 1 + j, []).append(lambda e=e: h_interleave(e))
+                h_jobs.setdefault(n + 2 + j, []).append(lambda e=e: h_output(e))
+                h_jobs.setdefault(n + 3 + j, []).insert(0, lambda e=e: store(e))
+
+        def h_output(e):
+            h_quantise(e)
+            bias2(e)
+            mm2(e)
+
+        def h_beat(n):
+            for job in h_jobs.pop(n, []):
+                job()
+
+        units = [(e, g) for e in range(E) for g in range(G)]
+        n_units = len(units)
+
+        def late(n, lag):
+            return units[n - lag] if 0 <= n - lag < n_units else None
+
+        for n in range(n_units + RELU_LAG + 4):
+            u = late(n, 0)
+            if u:
+                w2_widen(*u)
+            if n == 1:
+                x_quantise(0)
+            v = late(n, Q_LAG)
+            if v:
+                direct_quantise(*v)
+                direct_mm1(*v)
+            v = late(n, W_LAG)
+            if v:
+                w2_quantise(*v)
+            v = late(n, RELU_LAG)
+            if v:
+                for s in range(4):
+                    h_relu(*v, s)
+                if v[1] == G - 1:
+                    finish(n, [v[0]])
+            h_beat(n)
+            if u:
+                direct_interleave(*u)
+                if n == 0:
+                    x_turn(0)
+                w2_interleave(*u)
+                e, g = u
+                if e in (1, 2, 3) and g == 0:
+                    x_turn(e)
+                if e in (1, 2, 3) and g == 1:
+                    x_quantise(e)
+                if n == 3:
+                    gain_calc()
+                if n + 5 < n_units:
+                    load_direct(*units[n + 5])
+                if g % 2 == 1 and n + 5 < n_units:
+                    load_w2(units[n + 5][0], units[n + 5][1] // 2)
+                if g == 0:
+                    b2_load((e,))
+                if n == 1:
+                    nc.sync.dma_start(out=x_all[:, 2:8, :], in_=x_src[:, 2:8, :])

@@ -17,12 +17,11 @@ N, D, H, E = 1024, 512, 2048, 8
 P = 128
 TOK = N // E
 G = H // 512
-DRING = 8
-Q_LAG = 2
-W_LAG = 2
-RELU_LAG = 3
-D_ENG = "sssv"
-H_SPLIT = 0
+UNITS = E * G
+LEAD = 3
+RUN = 4
+AHEAD = 4
+S_WIDEN_FROM = UNITS - 2
 CLAMP_MAX = float(math.log(100.0))
 FLOPS = 2 * N * D * H * 2
 
@@ -30,131 +29,123 @@ FLOPS = 2 * N * D * H * 2
 def tile_moelayer_kernel(tc, x, W1, b1, W2_bytes, W2_scale, b2, temperature, out):
     nc = tc.nc
 
-    def split_copy(dst, src, s_part):
-        if s_part > 0:
-            nc.scalar.copy(out=dst[:, 0:s_part], in_=src[:, 0:s_part])
-        if s_part < dst.shape[1]:
-            nc.vector.tensor_copy(out=dst[:, s_part:dst.shape[1]], in_=src[:, s_part:dst.shape[1]])
-
-    def copy(engine, dst, src):
-        if engine == "v":
-            nc.vector.tensor_copy(out=dst, in_=src)
-        else:
-            nc.scalar.copy(out=dst, in_=src)
-
     with ExitStack() as ctx:
         ctx.enter_context(tc.manual_schedule())
         const = ctx.enter_context(tc.tile_pool(name="const", bufs=1))
-        raw_pool = ctx.enter_context(tc.tile_pool(name="raw_pool", bufs=2))
-        byte_pool = ctx.enter_context(tc.tile_pool(name="byte_pool", bufs=6))
+        raw_pool = ctx.enter_context(tc.tile_pool(name="raw_pool", bufs=AHEAD + 2))
+        byte_pool = ctx.enter_context(tc.tile_pool(name="byte_pool", bufs=AHEAD + 2))
         work = ctx.enter_context(tc.tile_pool(name="work", bufs=3))
-        grp_pool = ctx.enter_context(tc.tile_pool(name="grp_pool", bufs=4))
-        w2_codes = ctx.enter_context(tc.tile_pool(name="w2_codes", bufs=10))
-        hq_pool = ctx.enter_context(tc.tile_pool(name="hq_pool", bufs=3))
+        codes = ctx.enter_context(tc.tile_pool(name="codes", bufs=4))
         out_pool = ctx.enter_context(tc.tile_pool(name="out_pool", bufs=2))
         ps_t = ctx.enter_context(tc.psum_pool(name="ps_t", bufs=2))
         ps_h = ctx.enter_context(tc.psum_pool(name="ps_h", bufs=4))
         ps_y = ctx.enter_context(tc.psum_pool(name="ps_y", bufs=2))
 
-        w1_raw, w2_raw, b2_tile, turned = {}, {}, {}, {}
+        w1_raw, w2_raw, b2_row, b2_gain = {}, {}, {}, {}
+        w1_grp, w1_cod, w2_pl, w2_grp, w2_cod = {}, {}, {}, {}, {}
+        h_ps, h_pl, h_grp, h_cod, y_ps, x_grp = {}, {}, {}, {}, {}, {}
 
-        def load_direct(e, g):
-            raw = raw_pool.tile([P, 4, 512], BF16, name="raw_d", align_bytes=64, bufs=DRING)
+        def copy(engine, dst, src):
+            if engine == "v":
+                nc.vector.tensor_copy(out=dst, in_=src)
+            else:
+                nc.scalar.copy(out=dst, in_=src)
+
+        def quantise(name, grp, width):
+            q = codes.tile([P, width], U32, name=name + "_q", align_bytes=64)
+            sc = codes.tile([P, width], U8, name=name + "_s", align_bytes=64)
+            nc.vector.quantize_mx(out=q[:].bitcast(FP8X4), scales=sc[:], in_=grp)
+            return q, sc
+
+        def load_w1(u):
+            e, g = divmod(u, G)
+            raw = raw_pool.tile([P, 4, 512], BF16, name="w1_raw", align_bytes=64)
             nc.sync.dma_start(
                 out=raw[:], in_=W1[e].rearrange("(p j) n -> p j n", j=4)[:, :, g * 512:(g + 1) * 512]
             )
-            w1_raw[e, g] = raw
+            w1_raw[u] = raw
 
-        def load_w2(e, half):
-            wb = byte_pool.tile([P, 2, 2048], U8, name="wb", align_bytes=64)
-            src = W2_bytes[e].rearrange("(g p s) n -> p g (s n)", p=P, s=4)[:, 2 * half:2 * half + 2, :]
-            if e == 0 and half == 0:
-                for g in range(2):
-                    nc.sync.dma_start(out=wb[:, g, :], in_=src[:, g, :])
-            else:
-                nc.sync.dma_start(out=wb[:], in_=src)
-            w2_raw[e, half] = wb
+        def load_w2(u):
+            e, g = divmod(u, G)
+            wb = byte_pool.tile([P, 2048], U8, name="w2_bytes", align_bytes=64)
+            nc.sync.dma_start(
+                out=wb[:], in_=W2_bytes[e].rearrange("(g p s) n -> p g (s n)", p=P, s=4)[:, g, :]
+            )
+            w2_raw[u] = wb
 
-        rows = out_pool.tile([P, 512], F32, name="rows", tag="y", align_bytes=64)
-        nc.vector.memset(rows[:], 0.0)
-        nc.sync.dma_start(out=rows[32:36, :], in_=W2_scale.rearrange("o (g c) z -> (o g) (c z)", c=512))
-        b1_rows = out_pool.tile([32, 512], BF16, name="b1_rows", tag="b2_row", align_bytes=64, bufs=4)
-        nc.sync.dma_start(out=b1_rows[:], in_=b1.rearrange("e (g c) -> (e g) c", c=512))
-        load_direct(0, 0)
-        load_w2(0, 0)
-        load_w2(0, 1)
-        x_all = const.tile([P, E, D], BF16, name="x_all", align_bytes=64)
-        x_src = x.rearrange("(e p) d -> p e d", p=P)
-        nc.sync.dma_start(out=x_all[:, 0:2, :], in_=x_src[:, 0:2, :])
+        def load_b2(e):
+            row = out_pool.tile([P, D], BF16, name="b2_row", align_bytes=64)
+            nc.sync.dma_start(out=row[:], in_=b2[e, :].partition_broadcast(P))
+            b2_row[e] = row
+
         temp = const.tile([P, 1], BF16, name="temp", align_bytes=64)
-        nc.sync.dma_start(out=temp[:], in_=temperature.partition_broadcast(P))
-        for g in range(1, G):
-            load_direct(0, g)
-        load_w2(1, 0)
-        load_direct(1, 0)
+        w2_scale = const.tile([P, G, 4], F32, name="w2_scale", align_bytes=64)
+        b1_col = const.tile([P, UNITS, 4], BF16, name="b1_col", align_bytes=64)
+        x_head = const.tile([P, 2, D], BF16, name="x_head", align_bytes=64)
+        x_rest = const.tile([P, E - 2, D], BF16, name="x_rest", align_bytes=64)
+        x_src = x.rearrange("(e p) d -> p e d", p=P)
+
+        nc.scalar.dma_start(out=temp[:], in_=temperature.partition_broadcast(P))
+        load_w1(0)
+        load_w1(1)
+        nc.sync.dma_start(out=x_head[:], in_=x_src[:, 0:2, :])
+        load_w2(0)
+        nc.sync.dma_start(
+            out=w2_scale[:], in_=W2_scale.rearrange("o (g p s) z -> p g (o s z)", p=P, s=4)
+        )
+        load_w1(2)
+        nc.sync.dma_start(out=b1_col[:], in_=b1.rearrange("e (g p s) -> p (e g) s", p=P, s=4))
+        for u in range(1, AHEAD):
+            load_w1(u + LEAD - 1)
+            load_w2(u)
+        load_w1(AHEAD + LEAD - 1)
 
         ident = const.tile([P, P], F32, name="ident", align_bytes=64)
         make_identity(nc, ident[:])
 
-        nc.vector.tensor_copy(out=rows[0:32, :], in_=b1_rows[:])
-        rows_s = out_pool.tile([P, 4, P], F32, name="rows_s", tag="bg", align_bytes=64)
-        nc.vector.tensor_copy(out=rows_s[:], in_=rows[:].rearrange("r (m s) -> r s m", s=4))
-        col_ps = ps_t.tile([P, 4, P], F32, name="tp")
-        for s in range(4):
-            nc.tensor.transpose(col_ps[:, s, :], rows_s[:, s, :], ident[:])
-        cols = const.tile([P, 36, 4], F32, name="cols", align_bytes=64)
-        nc.vector.tensor_copy(out=cols[:], in_=col_ps[:, :, 0:36].rearrange("p s r -> p r s"))
+        clamped = const.tile([P, 1], F32, name="clamped", align_bytes=64)
+        gain = const.tile([P, 1], F32, name="gain", align_bytes=64)
+        nc.vector.tensor_scalar_min(clamped[:], temp[:], CLAMP_MAX)
+        nc.scalar.activation(out=gain[:], in_=clamped[:], func=ACT.Exp)
 
         xq = const.tile([P, E, TOK], U32, name="xq", align_bytes=64)
         xs = const.tile([P, E, TOK], U8, name="xs", align_bytes=64)
-        xg_t, gain = {}, const.tile([P, 1], F32, name="gain", align_bytes=64)
-
-        def gain_calc():
-            clamped = const.tile([P, 1], F32, name="clamped", align_bytes=64)
-            nc.vector.tensor_scalar_min(clamped[:], temp[:], CLAMP_MAX)
-            nc.scalar.activation(out=gain[:], in_=clamped[:], func=ACT.Exp)
 
         def x_turn(k):
             tp = ps_t.tile([P, 4, P], F32, name="tp")
             for i in range(2):
-                words = x_all[:, 2 * k + i, :].bitcast(F32)
+                rows = x_head[:, i, :] if k == 0 else x_rest[:, 2 * k - 2 + i, :]
+                words = rows.bitcast(F32)
                 for u in range(2):
                     nc.tensor.transpose(tp[:, 2 * i + u, :], words[:, u:256:2], ident[:])
-            xg = work.tile([P, 2, TOK, 4], BF16, name="xg", align_bytes=64, bufs=1)
-            for i in range(2):
-                copy("s", xg[:, i, :, :].bitcast(F32), tp[:, 2 * i:2 * i + 2, :].rearrange("p u r -> p r u"))
-            xg_t[k] = xg
+            xg = work.tile([P, 2, TOK, 4], BF16, name="xg", align_bytes=64, bufs=2)
+            nc.scalar.copy(
+                out=xg[:].bitcast(F32), in_=tp[:].rearrange("p (i u) r -> p i r u", u=2)
+            )
+            x_grp[k] = xg
 
         def x_quantise(k):
             nc.vector.quantize_mx(
                 out=xq[:, 2 * k:2 * k + 2, :].rearrange("p e r -> p (e r)").bitcast(FP8X4),
                 scales=xs[:, 2 * k:2 * k + 2, :].rearrange("p e r -> p (e r)"),
-                in_=xg_t[k][:].rearrange("p e r t -> p (e r t)"),
+                in_=x_grp[k][:].rearrange("p e r t -> p (e r t)"),
             )
 
-        w1_grp, w1_cod, w2_pl, w2_grp, w2_cod, h_ps, h_pl, h_grp, h_cod, y_ps, b2g = ({} for i in range(11))
-
-        def direct_interleave(e, g):
-            grp = grp_pool.tile([P, 4, P, 4], BF16, name="w1g", align_bytes=64)
-            src = w1_raw[e, g][:].rearrange("p j (m s) -> p m s j", s=4)
-            dst = grp[:].rearrange("p s m j -> p m s j")
-            if D_ENG[(G * e + g) % len(D_ENG)] == "v":
-                nc.vector.tensor_copy(out=dst, in_=src)
-            else:
-                nc.scalar.copy(out=dst, in_=src)
-            w1_grp[e, g] = grp
-
-        def direct_quantise(e, g):
-            q = grp_pool.tile([P, 512], U32, name="w1q", align_bytes=64)
-            sc = grp_pool.tile([P, 512], U8, name="w1s", align_bytes=64)
-            nc.vector.quantize_mx(
-                out=q[:].bitcast(FP8X4), scales=sc[:],
-                in_=w1_grp[e, g][:].rearrange("p s m j -> p (s m j)"),
+        def w1_interleave(u, engine):
+            grp = work.tile([P, 4, P, 4], BF16, name="w1_grp", align_bytes=64, bufs=4)
+            copy(
+                engine,
+                grp[:].rearrange("p s m j -> p m j s"),
+                w1_raw[u][:].rearrange("p j (m s) -> p m j s", s=4),
             )
-            w1_cod[e, g] = (q, sc)
+            w1_grp[u] = grp
 
-        def direct_mm1(e, g):
-            q, sc = w1_cod[e, g]
+        def w1_quantise(u):
+            w1_cod[u] = quantise("w1", w1_grp[u][:].rearrange("p s m j -> p (s m j)"), 512)
+
+        def mm1(u):
+            e = u // G
+            q, sc = w1_cod[u]
             ph = ps_h.tile([P, 4, TOK], F32, name="ph")
             for s in range(4):
                 nc.tensor.matmul_mx(
@@ -163,152 +154,122 @@ def tile_moelayer_kernel(tc, x, W1, b1, W2_bytes, W2_scale, b2, temperature, out
                     rhs=xq[:, e, :].bitcast(FP8X4), rhs_scale=xs[:, e, :],
                     start=True, stop=True,
                 )
+            h_ps[u] = ph
+
+        def h_relu(u):
+            pl = work.tile([P, 4, TOK], BF16, name="h_pl", align_bytes=64)
             for s in range(4):
-                h_ps[e, g, s] = ph[:, s, :]
-
-        def h_relu(e, g, s):
-            if e not in h_pl:
-                h_pl[e] = work.tile([P, 4, G * TOK], BF16, name="hp", align_bytes=64, bufs=4)
-            nc.scalar.activation(
-                out=h_pl[e][:, s, g * TOK:(g + 1) * TOK], in_=h_ps[e, g, s],
-                func=ACT.Relu, bias=cols[:, 4 * e + g, s:s + 1],
-            )
-
-        def h_interleave(e):
-            grp = work.tile([P, G * TOK, 4], BF16, name="hg", align_bytes=64, bufs=2)
-            split_copy(
-                grp[:].rearrange("p (c i) s -> p c s i", i=4),
-                h_pl[e][:].rearrange("p s (c i) -> p c s i", i=4),
-                64 if e >= 6 else H_SPLIT,
-            )
-            h_grp[e] = grp
-
-        def h_quantise(e):
-            q = hq_pool.tile([P, G * TOK], U32, name="hq", align_bytes=64)
-            sc = hq_pool.tile([P, G * TOK], U8, name="hs", align_bytes=64)
-            nc.vector.quantize_mx(
-                out=q[:].bitcast(FP8X4), scales=sc[:], in_=h_grp[e][:].rearrange("p n s -> p (n s)")
-            )
-            h_cod[e] = (q, sc)
-
-        def w2_widen(e, g):
-            plane = work.tile([P, 2, 512, 2], BF16, name="w2p", align_bytes=64, bufs=3)
-            for s in (0, 2, 1, 3):
-                nc.vector.tensor_scalar(
-                    out=plane[:, s // 2, :, s % 2],
-                    in0=w2_raw[e, g // 2][:, g % 2, s * 512:(s + 1) * 512].bitcast(FP8),
-                    scalar1=cols[:, 32 + g, s:s + 1], scalar2=None, op0=ALU.mult,
+                nc.scalar.activation(
+                    out=pl[:, s, :], in_=h_ps[u][:, s, :], func=ACT.Relu, bias=b1_col[:, u, s:s + 1]
                 )
-            w2_pl[e, g] = plane
+            h_pl[u] = pl
 
-        def w2_interleave(e, g):
-            grp = work.tile([P, 512, 4], BF16, name="w2g", align_bytes=64, bufs=4)
-            nc.scalar.copy(
-                out=grp[:].bitcast(F32),
-                in_=w2_pl[e, g][:].rearrange("p h n l -> p h (n l)").bitcast(F32).rearrange("p h n -> p n h"),
+        def interleave(engine, grp, planes):
+            copy(
+                engine,
+                grp.rearrange("p (c i) s -> p c s i", i=RUN),
+                planes.rearrange("p s (c i) -> p c s i", i=RUN),
             )
-            w2_grp[e, g] = grp
 
-        def w2_quantise(e, g):
-            q = w2_codes.tile([P, 512], U32, name="w2q", align_bytes=64)
-            sc = w2_codes.tile([P, 512], U8, name="w2s", align_bytes=64)
-            nc.vector.quantize_mx(
-                out=q[:].bitcast(FP8X4), scales=sc[:], in_=w2_grp[e, g][:].rearrange("p n s -> p (n s)")
+        def h_interleave(u):
+            grp = work.tile([P, TOK, 4], BF16, name="h_grp", align_bytes=64)
+            interleave("s", grp[:], h_pl[u][:])
+            h_grp[u] = grp
+
+        def h_quantise(u):
+            h_cod[u] = quantise("h", h_grp[u][:].rearrange("p n s -> p (n s)"), TOK)
+
+        def w2_widen(u, engine):
+            g = u % G
+            pl = work.tile([P, 4, 512], BF16, name="w2_pl", align_bytes=64)
+            for s in range(4):
+                src = w2_raw[u][:, s * 512:(s + 1) * 512].bitcast(FP8)
+                if engine == "v":
+                    nc.vector.tensor_scalar(
+                        out=pl[:, s, :], in0=src, scalar1=w2_scale[:, g, s:s + 1], scalar2=None,
+                        op0=ALU.mult,
+                    )
+                else:
+                    nc.scalar.activation(
+                        out=pl[:, s, :], in_=src, func=ACT.Copy, scale=w2_scale[:, g, s:s + 1]
+                    )
+            w2_pl[u] = pl
+
+        def w2_interleave(u):
+            grp = work.tile([P, 512, 4], BF16, name="w2_grp", align_bytes=64)
+            interleave("v", grp[:], w2_pl[u][:])
+            w2_grp[u] = grp
+
+        def w2_quantise(u):
+            w2_cod[u] = quantise("w2", w2_grp[u][:].rearrange("p n s -> p (n s)"), 512)
+
+        def mm2(u):
+            e, g = divmod(u, G)
+            if g == 0:
+                y_ps[e] = ps_y.tile([TOK, D], F32, name="py")
+            hq, hs = h_cod[u]
+            wq, ws = w2_cod[u]
+            nc.tensor.matmul_mx(
+                out=y_ps[e][:], lhsT=hq[:].bitcast(FP8X4), lhsT_scale=hs[:],
+                rhs=wq[:].bitcast(FP8X4), rhs_scale=ws[:],
+                start=(g == 0), stop=(g == G - 1),
             )
-            w2_cod[e, g] = (q, sc)
-
-        def mm2(e):
-            py = ps_y.tile([TOK, D], F32, name="py")
-            hq, hs = h_cod[e]
-            for g in range(G):
-                wq, ws = w2_cod[e, g]
-                c = slice(g * TOK, (g + 1) * TOK)
-                nc.tensor.matmul_mx(
-                    out=py[:], lhsT=hq[:, c].bitcast(FP8X4), lhsT_scale=hs[:, c],
-                    rhs=wq[:].bitcast(FP8X4), rhs_scale=ws[:],
-                    start=(g == 0), stop=(g == G - 1),
-                )
-            y_ps[e] = py
-
-        def b2_load(experts):
-            for e in experts:
-                b2_tile[e] = out_pool.tile([P, D], BF16, name="b2_row", align_bytes=64, bufs=4)
-                nc.sync.dma_start(out=b2_tile[e][:], in_=b2[e, :].partition_broadcast(P))
 
         def bias2(e):
-            bg = out_pool.tile([P, D], F32, name="bg", align_bytes=64)
+            bg = out_pool.tile([P, D], F32, name="b2_gain", align_bytes=64)
             nc.vector.tensor_scalar(
-                out=bg[:], in0=b2_tile[e][:], scalar1=gain[:], scalar2=None, op0=ALU.mult
+                out=bg[:], in0=b2_row[e][:], scalar1=gain[:], scalar2=None, op0=ALU.mult
             )
-            b2g[e] = bg
+            b2_gain[e] = bg
 
         def store(e):
             y = out_pool.tile([TOK, D], F32, name="y", align_bytes=64)
             nc.vector.scalar_tensor_tensor(
-                out=y[:], in0=y_ps[e][:], scalar=gain[:], in1=b2g[e][:], op0=ALU.mult, op1=ALU.add
+                out=y[:], in0=y_ps[e][:], scalar=gain[:], in1=b2_gain[e][:], op0=ALU.mult, op1=ALU.add
             )
             nc.sync.dma_start(out=out[e * TOK:(e + 1) * TOK, :], in_=y[:])
 
-        h_jobs = {}
+        def live(u):
+            return 0 <= u < UNITS
 
-        def finish(n, experts):
-            for j, e in enumerate(experts):
-                h_jobs.setdefault(n + 1 + j, []).append(lambda e=e: h_interleave(e))
-                h_jobs.setdefault(n + 2 + j, []).append(lambda e=e: h_output(e))
-                h_jobs.setdefault(n + 3 + j, []).insert(0, lambda e=e: store(e))
-
-        def h_output(e):
-            h_quantise(e)
-            bias2(e)
-            mm2(e)
-
-        def h_beat(n):
-            for job in h_jobs.pop(n, []):
-                job()
-
-        units = [(e, g) for e in range(E) for g in range(G)]
-        n_units = len(units)
-
-        def late(n, lag):
-            return units[n - lag] if 0 <= n - lag < n_units else None
-
-        for n in range(n_units + RELU_LAG + 4):
-            u = late(n, 0)
-            if u:
-                w2_widen(*u)
-            if n == 1:
-                x_quantise(0)
-            v = late(n, Q_LAG)
-            if v:
-                direct_quantise(*v)
-                direct_mm1(*v)
-            v = late(n, W_LAG)
-            if v:
-                w2_quantise(*v)
-            v = late(n, RELU_LAG)
-            if v:
-                for s in range(4):
-                    h_relu(*v, s)
-                if v[1] == G - 1:
-                    finish(n, [v[0]])
-            h_beat(n)
-            if u:
-                direct_interleave(*u)
-                if n == 0:
-                    x_turn(0)
-                w2_interleave(*u)
-                e, g = u
-                if e in (1, 2, 3) and g == 0:
-                    x_turn(e)
-                if e in (1, 2, 3) and g == 1:
-                    x_quantise(e)
-                if n == 3:
-                    gain_calc()
-                if n + 5 < n_units:
-                    load_direct(*units[n + 5])
-                if g % 2 == 1 and n + 5 < n_units:
-                    load_w2(units[n + 5][0], units[n + 5][1] // 2)
-                if g == 0:
-                    b2_load((e,))
-                if n == 1:
-                    nc.sync.dma_start(out=x_all[:, 2:8, :], in_=x_src[:, 2:8, :])
+        for n in range(-LEAD, UNITS + 2):
+            u = n + LEAD
+            if live(n) and n < S_WIDEN_FROM:
+                w2_widen(n, "v")
+            if live(n - 1):
+                w2_quantise(n - 1)
+                mm2(n - 1)
+            if u in (2, 6, 14, 22):
+                x_quantise((u + 2) // 8 if u > 2 else 0)
+            if u == 2:
+                w1_quantise(0)
+                mm1(0)
+            if live(u - 1) and u != 1:
+                w1_quantise(u - 1)
+                mm1(u - 1)
+            if live(u - 2):
+                h_relu(u - 2)
+            if live(u):
+                w1_interleave(u, "v" if u == 1 else "s")
+            if S_WIDEN_FROM <= n + 1 < UNITS:
+                w2_widen(n + 1, "s")
+            if u in (0, 5, 13, 21):
+                x_turn((u + 3) // 8)
+            if live(u - 2):
+                h_interleave(u - 2)
+            if live(n):
+                w2_interleave(n)
+            if live(u - 3):
+                h_quantise(u - 3)
+            if live(n) and n % G == 2:
+                bias2(n // G)
+            if live(n - 2) and (n - 2) % G == G - 1:
+                store((n - 2) // G)
+            if n >= 0 and live(n + AHEAD):
+                load_w2(n + AHEAD)
+            if n >= 0 and live(u + AHEAD):
+                load_w1(u + AHEAD)
+            if live(n) and n % G == 0:
+                load_b2(n // G)
+            if n == 0:
+                nc.sync.dma_start(out=x_rest[:], in_=x_src[:, 2:E, :])

@@ -18,10 +18,11 @@ P = 128
 TOK = N // E
 G = H // 512
 UNITS = E * G
-LEAD = 3
+CATCH_UP = (4, 12)
 RUN = 4
 AHEAD = 4
-S_WIDEN_FROM = UNITS - 2
+S_SLICES = 3
+PARK = (E - 1) * TOK
 CLAMP_MAX = float(math.log(100.0))
 FLOPS = 2 * N * D * H * 2
 
@@ -32,18 +33,21 @@ def tile_moelayer_kernel(tc, x, W1, b1, W2_bytes, W2_scale, b2, temperature, out
     with ExitStack() as ctx:
         ctx.enter_context(tc.manual_schedule())
         const = ctx.enter_context(tc.tile_pool(name="const", bufs=1))
-        raw_pool = ctx.enter_context(tc.tile_pool(name="raw_pool", bufs=AHEAD + 2))
+        raw_pool = ctx.enter_context(tc.tile_pool(name="raw_pool", bufs=AHEAD + 4))
         byte_pool = ctx.enter_context(tc.tile_pool(name="byte_pool", bufs=AHEAD + 2))
         work = ctx.enter_context(tc.tile_pool(name="work", bufs=3))
-        codes = ctx.enter_context(tc.tile_pool(name="codes", bufs=4))
+        codes = ctx.enter_context(tc.tile_pool(name="codes", bufs=6))
         out_pool = ctx.enter_context(tc.tile_pool(name="out_pool", bufs=2))
         ps_t = ctx.enter_context(tc.psum_pool(name="ps_t", bufs=2))
         ps_h = ctx.enter_context(tc.psum_pool(name="ps_h", bufs=4))
         ps_y = ctx.enter_context(tc.psum_pool(name="ps_y", bufs=2))
 
-        w1_raw, w2_raw, b2_row, b2_gain = {}, {}, {}, {}
-        w1_grp, w1_cod, w2_pl, w2_grp, w2_cod = {}, {}, {}, {}, {}
-        h_ps, h_pl, h_grp, h_cod, y_ps, x_grp = {}, {}, {}, {}, {}, {}
+        w1_raw, w2_raw, b1_col, b2_gain = {}, {}, {}, {}
+        pair, w1_cod, w2_pl, w2_cod = {}, {}, {}, {}
+        h_ps, h_pl, h_grp, h_cod, y_ps, x_grp, x_ps = {}, {}, {}, {}, {}, {}, {}
+
+        def live(u):
+            return 0 <= u < UNITS
 
         def copy(engine, dst, src):
             if engine == "v":
@@ -57,13 +61,16 @@ def tile_moelayer_kernel(tc, x, W1, b1, W2_bytes, W2_scale, b2, temperature, out
             nc.vector.quantize_mx(out=q[:].bitcast(FP8X4), scales=sc[:], in_=grp)
             return q, sc
 
-        def load_w1(u):
+        def load_w1(u, parts=1):
             e, g = divmod(u, G)
-            raw = raw_pool.tile([P, 4, 512], BF16, name="w1_raw", align_bytes=64)
-            nc.sync.dma_start(
-                out=raw[:], in_=W1[e].rearrange("(p j) n -> p j n", j=4)[:, :, g * 512:(g + 1) * 512]
-            )
-            w1_raw[u] = raw
+            width = 512 // parts
+            for a in range(parts):
+                raw = raw_pool.tile([P, 4, width], BF16, name="w1_raw", align_bytes=64)
+                c0 = g * 512 + a * width
+                nc.sync.dma_start(
+                    out=raw[:], in_=W1[e].rearrange("(p j) n -> p j n", j=4)[:, :, c0:c0 + width]
+                )
+                w1_raw.setdefault(u, []).append(raw)
 
         def load_w2(u):
             e, g = divmod(u, G)
@@ -73,32 +80,43 @@ def tile_moelayer_kernel(tc, x, W1, b1, W2_bytes, W2_scale, b2, temperature, out
             )
             w2_raw[u] = wb
 
+        def load_b1(e):
+            col = out_pool.tile([P, G, 16], BF16, name="b1_col", align_bytes=64, bufs=3)
+            nc.sync.dma_start(out=col[:, :, 0:4], in_=b1[e].rearrange("(g p s) -> p g s", p=P, s=4))
+            b1_col[e] = col
+
         def load_b2(e):
-            row = out_pool.tile([P, D], BF16, name="b2_row", align_bytes=64)
-            nc.sync.dma_start(out=row[:], in_=b2[e, :].partition_broadcast(P))
-            b2_row[e] = row
+            row = out_pool.tile([P, D], F32, name="b2_gain", align_bytes=64, bufs=3)
+            nc.sync.dma_start(out=row[:], in_=out[PARK + e, :].partition_broadcast(P))
+            b2_gain[e] = row
 
         temp = const.tile([P, 1], BF16, name="temp", align_bytes=64)
-        w2_scale = const.tile([P, G, 4], F32, name="w2_scale", align_bytes=64)
-        b1_col = const.tile([P, UNITS, 4], BF16, name="b1_col", align_bytes=64)
+        scale_head = const.tile([P, 4], F32, name="scale_head", align_bytes=64)
+        scale_rest = const.tile([P, G - 1, 8], F32, name="scale_rest", align_bytes=64)
         x_head = const.tile([P, 2, D], BF16, name="x_head", align_bytes=64)
         x_rest = const.tile([P, E - 2, D], BF16, name="x_rest", align_bytes=64)
+        b2_rows = const.tile([E, D], BF16, name="b2_rows", align_bytes=64)
         x_src = x.rearrange("(e p) d -> p e d", p=P)
+        scale_src = W2_scale.rearrange("o (g p s) z -> p g (o s z)", p=P, s=4)
 
-        nc.scalar.dma_start(out=temp[:], in_=temperature.partition_broadcast(P))
-        load_w1(0)
+        def w2_scale(g, s):
+            return scale_head[:, s:s + 1] if g == 0 else scale_rest[:, g - 1, s:s + 1]
+
+        nc.sync.dma_start(out=temp[:], in_=temperature.partition_broadcast(P))
+        nc.sync.dma_start(out=scale_head[:], in_=scale_src[:, 0, :])
+        load_w2(0)
+        load_w1(0, parts=2)
+        load_w2(1)
+        nc.sync.dma_start(out=scale_rest[:, :, 0:4], in_=scale_src[:, 1:G, :])
         load_w1(1)
         nc.sync.dma_start(out=x_head[:], in_=x_src[:, 0:2, :])
-        load_w2(0)
-        nc.sync.dma_start(
-            out=w2_scale[:], in_=W2_scale.rearrange("o (g p s) z -> p g (o s z)", p=P, s=4)
-        )
+        load_w2(2)
         load_w1(2)
-        nc.sync.dma_start(out=b1_col[:], in_=b1.rearrange("e (g p s) -> p (e g) s", p=P, s=4))
-        for u in range(1, AHEAD):
-            load_w1(u + LEAD - 1)
+        load_b1(0)
+        nc.sync.dma_start(out=b2_rows[:], in_=b2)
+        for u in range(3, AHEAD):
             load_w2(u)
-        load_w1(AHEAD + LEAD - 1)
+            load_w1(u)
 
         ident = const.tile([P, P], F32, name="ident", align_bytes=64)
         make_identity(nc, ident[:])
@@ -107,6 +125,13 @@ def tile_moelayer_kernel(tc, x, W1, b1, W2_bytes, W2_scale, b2, temperature, out
         gain = const.tile([P, 1], F32, name="gain", align_bytes=64)
         nc.vector.tensor_scalar_min(clamped[:], temp[:], CLAMP_MAX)
         nc.scalar.activation(out=gain[:], in_=clamped[:], func=ACT.Exp)
+
+        def park_b2():
+            rows = const.tile([E, D], F32, name="b2_scaled", align_bytes=64)
+            nc.vector.tensor_scalar(
+                out=rows[:], in0=b2_rows[:], scalar1=gain[0:E, :], scalar2=None, op0=ALU.mult
+            )
+            nc.sync.dma_start(out=out[PARK:PARK + E, :], in_=rows[:])
 
         xq = const.tile([P, E, TOK], U32, name="xq", align_bytes=64)
         xs = const.tile([P, E, TOK], U8, name="xs", align_bytes=64)
@@ -118,6 +143,10 @@ def tile_moelayer_kernel(tc, x, W1, b1, W2_bytes, W2_scale, b2, temperature, out
                 words = rows.bitcast(F32)
                 for u in range(2):
                     nc.tensor.transpose(tp[:, 2 * i + u, :], words[:, u:256:2], ident[:])
+            x_ps[k] = tp
+
+        def x_copy(k):
+            tp = x_ps[k]
             xg = work.tile([P, 2, TOK, 4], BF16, name="xg", align_bytes=64, bufs=2)
             nc.scalar.copy(
                 out=xg[:].bitcast(F32), in_=tp[:].rearrange("p (i u) r -> p i r u", u=2)
@@ -131,17 +160,43 @@ def tile_moelayer_kernel(tc, x, W1, b1, W2_bytes, W2_scale, b2, temperature, out
                 in_=x_grp[k][:].rearrange("p e r t -> p (e r t)"),
             )
 
-        def w1_interleave(u, engine):
-            grp = work.tile([P, 4, P, 4], BF16, name="w1_grp", align_bytes=64, bufs=4)
-            copy(
-                engine,
-                grp[:].rearrange("p s m j -> p m j s"),
-                w1_raw[u][:].rearrange("p j (m s) -> p m j s", s=4),
-            )
-            w1_grp[u] = grp
+        def slot(b, kind, u):
+            if b not in pair:
+                pair[b] = (work.tile([P, 2, 2048], BF16, name="w_grp", align_bytes=64, bufs=4), [])
+            tile, held = pair[b]
+            held.append((kind, u))
+            return tile[:, len(held) - 1, :]
 
-        def w1_quantise(u):
-            w1_cod[u] = quantise("w1", w1_grp[u][:].rearrange("p s m j -> p (s m j)"), 512)
+        def w1_interleave(u, engine, dst):
+            grp = dst.rearrange("p (s m j) -> p m j s", s=4, j=4)
+            width = P // len(w1_raw[u])
+            for a, raw in enumerate(w1_raw[u]):
+                copy(
+                    engine,
+                    grp[:, a * width:(a + 1) * width],
+                    raw[:].rearrange("p j (m s) -> p m j s", s=4),
+                )
+
+        def pair_quantise(b):
+            tile, held = pair[b]
+            q, sc = quantise("w", tile[:, 0:len(held), :].rearrange("p a c -> p (a c)"), 512 * len(held))
+            for a, (kind, u) in enumerate(held):
+                kind[u] = (q[:, 512 * a:512 * (a + 1)], sc[:, 512 * a:512 * (a + 1)])
+
+        def last_unit(b):
+            u = UNITS - 1
+            tile = slot(b, w2_cod, u).rearrange("p (n s) -> p n s", s=4)
+            for a in range(2):
+                cols = slice(a * 256, (a + 1) * 256)
+                interleave("vs"[a], tile[:, cols, :], w2_pl[u][:, :, cols])
+            h_quantise(u)
+            halves = [
+                quantise("w", tile[:, a * 256:(a + 1) * 256, :].rearrange("p n s -> p (n s)"), 256)
+                for a in range(2)
+            ]
+            for a in range(2):
+                mm2_part(u, a, halves[a][0][:], halves[a][1][:])
+            store(E - 1)
 
         def mm1(u):
             e = u // G
@@ -160,7 +215,7 @@ def tile_moelayer_kernel(tc, x, W1, b1, W2_bytes, W2_scale, b2, temperature, out
             pl = work.tile([P, 4, TOK], BF16, name="h_pl", align_bytes=64)
             for s in range(4):
                 nc.scalar.activation(
-                    out=pl[:, s, :], in_=h_ps[u][:, s, :], func=ACT.Relu, bias=b1_col[:, u, s:s + 1]
+                    out=pl[:, s, :], in_=h_ps[u][:, s, :], func=ACT.Relu, bias=b1_col[u // G][:, u % G, s:s + 1]
                 )
             h_pl[u] = pl
 
@@ -171,105 +226,143 @@ def tile_moelayer_kernel(tc, x, W1, b1, W2_bytes, W2_scale, b2, temperature, out
                 planes.rearrange("p s (c i) -> p c s i", i=RUN),
             )
 
-        def h_interleave(u):
+        def h_interleave(u, engine):
             grp = work.tile([P, TOK, 4], BF16, name="h_grp", align_bytes=64)
-            interleave("s", grp[:], h_pl[u][:])
+            interleave(engine, grp[:], h_pl[u][:])
             h_grp[u] = grp
 
         def h_quantise(u):
             h_cod[u] = quantise("h", h_grp[u][:].rearrange("p n s -> p (n s)"), TOK)
 
-        def w2_widen(u, engine):
+        def w2_widen(u, engine, slots):
             g = u % G
-            pl = work.tile([P, 4, 512], BF16, name="w2_pl", align_bytes=64)
-            for s in range(4):
+            if u not in w2_pl:
+                w2_pl[u] = work.tile([P, 4, 512], BF16, name="w2_pl", align_bytes=64)
+            pl = w2_pl[u]
+            for s in slots:
                 src = w2_raw[u][:, s * 512:(s + 1) * 512].bitcast(FP8)
                 if engine == "v":
                     nc.vector.tensor_scalar(
-                        out=pl[:, s, :], in0=src, scalar1=w2_scale[:, g, s:s + 1], scalar2=None,
+                        out=pl[:, s, :], in0=src, scalar1=w2_scale(g, s), scalar2=None,
                         op0=ALU.mult,
                     )
                 else:
                     nc.scalar.activation(
-                        out=pl[:, s, :], in_=src, func=ACT.Copy, scale=w2_scale[:, g, s:s + 1]
+                        out=pl[:, s, :], in_=src, func=ACT.Copy, scale=w2_scale(g, s)
                     )
-            w2_pl[u] = pl
 
-        def w2_interleave(u):
-            grp = work.tile([P, 512, 4], BF16, name="w2_grp", align_bytes=64)
-            interleave("v", grp[:], w2_pl[u][:])
-            w2_grp[u] = grp
+        def w2_interleave(u, dst):
+            interleave("v", dst.rearrange("p (n s) -> p n s", s=4), w2_pl[u][:])
 
-        def w2_quantise(u):
-            w2_cod[u] = quantise("w2", w2_grp[u][:].rearrange("p n s -> p (n s)"), 512)
-
-        def mm2(u):
+        def mm2_part(u, a, wq, ws):
             e, g = divmod(u, G)
-            if g == 0:
-                y_ps[e] = ps_y.tile([TOK, D], F32, name="py")
             hq, hs = h_cod[u]
-            wq, ws = w2_cod[u]
             nc.tensor.matmul_mx(
-                out=y_ps[e][:], lhsT=hq[:].bitcast(FP8X4), lhsT_scale=hs[:],
-                rhs=wq[:].bitcast(FP8X4), rhs_scale=ws[:],
+                out=y_ps[e][a][:], lhsT=hq[:].bitcast(FP8X4), lhsT_scale=hs[:],
+                rhs=wq.bitcast(FP8X4), rhs_scale=ws,
                 start=(g == 0), stop=(g == G - 1),
             )
 
-        def bias2(e):
-            bg = out_pool.tile([P, D], F32, name="b2_gain", align_bytes=64)
-            nc.vector.tensor_scalar(
-                out=bg[:], in0=b2_row[e][:], scalar1=gain[:], scalar2=None, op0=ALU.mult
-            )
-            b2_gain[e] = bg
+        def mm2(u):
+            e, g = divmod(u, G)
+            if g == 0 and e < E - 1:
+                y_ps[e] = [ps_y.tile([TOK, D], F32, name="py")]
+            if g == 0 and e == E - 1:
+                y_ps[e] = [ps_y.tile([TOK, 256], F32, name="py"), ps_t.tile([TOK, 256], F32, name="tp")]
+            wq, ws = w2_cod[u]
+            width = D // len(y_ps[e])
+            for a in range(len(y_ps[e])):
+                cols = slice(a * width, (a + 1) * width)
+                mm2_part(u, a, wq[:, cols], ws[:, cols])
 
         def store(e):
-            y = out_pool.tile([TOK, D], F32, name="y", align_bytes=64)
-            nc.vector.scalar_tensor_tensor(
-                out=y[:], in0=y_ps[e][:], scalar=gain[:], in1=b2_gain[e][:], op0=ALU.mult, op1=ALU.add
-            )
-            nc.sync.dma_start(out=out[e * TOK:(e + 1) * TOK, :], in_=y[:])
+            width = D // len(y_ps[e])
+            for a, py in enumerate(y_ps[e]):
+                cols = slice(a * width, (a + 1) * width)
+                y = out_pool.tile([TOK, width], F32, name="y", align_bytes=64, bufs=3)
+                nc.vector.scalar_tensor_tensor(
+                    out=y[:], in0=py[:], scalar=gain[:], in1=b2_gain[e][:, cols],
+                    op0=ALU.mult, op1=ALU.add,
+                )
+                nc.sync.dma_start(out=out[e * TOK:(e + 1) * TOK, cols], in_=y[:])
 
-        def live(u):
-            return 0 <= u < UNITS
+        plan, u1, u2 = [], 0, 0
+        while u2 < UNITS:
+            if len(plan) in CATCH_UP:
+                plan.append(([u1, u1 + 1], None))
+                u1 += 2
+            else:
+                plan.append(([u1] if u1 < UNITS else [], u2))
+                u1, u2 = min(u1 + 1, UNITS), u2 + 1
+        beats = len(plan)
 
-        for n in range(-LEAD, UNITS + 2):
-            u = n + LEAD
-            if live(n) and n < S_WIDEN_FROM:
-                w2_widen(n, "v")
-            if live(n - 1):
-                w2_quantise(n - 1)
-                mm2(n - 1)
-            if u in (2, 6, 14, 22):
-                x_quantise((u + 2) // 8 if u > 2 else 0)
-            if u == 2:
-                w1_quantise(0)
+        def w1_of(b):
+            return plan[b][0] if 0 <= b < beats else []
+
+        def w2_of(b):
+            return plan[b][1] if 0 <= b < beats else None
+
+        done_before, y_next, stored = 0, 0, 0
+        for b in range(beats):
+            w2 = w2_of(b)
+            catch_up = len(w1_of(b)) == 2
+            shared = w2 is not None and not w1_of(b - 1) and b > 0
+            if w2 is not None:
+                w2_widen(w2, "v", range(S_SLICES if shared else 0, 4))
+            if catch_up:
+                w1_interleave(w1_of(b)[0], "v", slot(b, w1_cod, w1_of(b)[0]))
+            for u in w1_of(b - 4):
+                if u < UNITS - 1:
+                    h_quantise(u)
+            for u in w1_of(b - 1):
+                if u == 1 or u % 8 == 7 and u + 1 < UNITS:
+                    x_quantise((u + 1) // 8)
+            if b - 1 in pair:
+                pair_quantise(b - 1)
+            if b == 2:
                 mm1(0)
-            if live(u - 1) and u != 1:
-                w1_quantise(u - 1)
-                mm1(u - 1)
-            if live(u - 2):
-                h_relu(u - 2)
-            if live(u):
-                w1_interleave(u, "v" if u == 1 else "s")
-            if S_WIDEN_FROM <= n + 1 < UNITS:
-                w2_widen(n + 1, "s")
-            if u in (0, 5, 13, 21):
-                x_turn((u + 3) // 8)
-            if live(u - 2):
-                h_interleave(u - 2)
-            if live(n):
-                w2_interleave(n)
-            if live(u - 3):
-                h_quantise(u - 3)
-            if live(n) and n % G == 2:
-                bias2(n // G)
-            if live(n - 2) and (n - 2) % G == G - 1:
-                store((n - 2) // G)
-            if n >= 0 and live(n + AHEAD):
-                load_w2(n + AHEAD)
-            if n >= 0 and live(u + AHEAD):
-                load_w1(u + AHEAD)
-            if live(n) and n % G == 0:
-                load_b2(n // G)
-            if n == 0:
+            for u in w1_of(b - 1):
+                if u > 0:
+                    mm1(u)
+            while y_next in h_cod and y_next in w2_cod:
+                mm2(y_next)
+                y_next += 1
+            for u in w1_of(b + 1):
+                if u % 8 == 6 and u + 2 < UNITS:
+                    x_turn((u + 2) // 8)
+            if b == 1:
+                x_turn(0)
+            if w2 is not None and b < beats - 1:
+                dst2 = slot(b, w2_cod, w2)
+            if w1_of(b):
+                w1_interleave(w1_of(b)[-1], "s", slot(b, w1_cod, w1_of(b)[-1]))
+            elif w2_of(b + 1) is not None:
+                w2_widen(w2_of(b + 1), "s", range(S_SLICES))
+            for u in w1_of(b):
+                if u == 1 or u % 8 == 6 and u + 2 < UNITS:
+                    x_copy((u + 2) // 8)
+            for u in w1_of(b - 3):
+                h_interleave(u, "v" if catch_up else "s")
+            for u in w1_of(b - 2):
+                h_relu(u)
+            if w2 is not None and b < beats - 1:
+                w2_interleave(w2, dst2)
+            if b == 2:
+                park_b2()
+            if stored < done_before:
+                store(stored)
+                stored += 1
+            done_before = y_next // G
+            if w2_of(b + AHEAD) is not None:
+                load_w2(w2_of(b + AHEAD))
+            for u in w1_of(b + AHEAD):
+                load_w1(u)
+                if u % G == 0:
+                    load_b1(u // G)
+            if b == 3:
+                load_b2(0)
+            if b % G == 1 and 0 < b // G < E:
+                load_b2(b // G)
+            if b == 0:
                 nc.sync.dma_start(out=x_rest[:], in_=x_src[:, 2:E, :])
+        last_unit(beats - 1)

@@ -18,7 +18,8 @@ P = 128
 TOK = N // E
 G = H // 512
 UNITS = E * G
-CATCH_UP = (4, 12)
+CATCH_UP = (4, 10)
+PE_SLICES = 1
 RUN = 4
 AHEAD = 4
 S_SLICES = 3
@@ -44,7 +45,7 @@ def tile_moelayer_kernel(tc, x, W1, b1, W2_bytes, W2_scale, b2, temperature, out
 
         w1_raw, w2_raw, b1_col, b2_gain = {}, {}, {}, {}
         pair, w1_cod, w2_pl, w2_cod = {}, {}, {}, {}
-        h_ps, h_pl, h_grp, h_cod, y_ps, x_grp, x_ps = {}, {}, {}, {}, {}, {}, {}
+        h_ps, h_pl, h_grp, h_cod, y_ps, x_grp, x_ps, w1_ps = {}, {}, {}, {}, {}, {}, {}, {}
 
         def live(u):
             return 0 <= u < UNITS
@@ -120,6 +121,8 @@ def tile_moelayer_kernel(tc, x, W1, b1, W2_bytes, W2_scale, b2, temperature, out
 
         ident = const.tile([P, P], F32, name="ident", align_bytes=64)
         make_identity(nc, ident[:])
+        ident_bf = const.tile([P, P], BF16, name="ident_bf", align_bytes=64)
+        make_identity(nc, ident_bf[:])
 
         clamped = const.tile([P, 1], F32, name="clamped", align_bytes=64)
         gain = const.tile([P, 1], F32, name="gain", align_bytes=64)
@@ -175,6 +178,27 @@ def tile_moelayer_kernel(tc, x, W1, b1, W2_bytes, W2_scale, b2, temperature, out
                     engine,
                     grp[:, a * width:(a + 1) * width],
                     raw[:].rearrange("p j (m s) -> p m j s", s=4),
+                )
+
+        def by_pe(u):
+            return u % 4 == 0 and u >= 8
+
+        def w1_to_psum(u):
+            src = w1_raw[u][0][:].rearrange("p j (m s) -> p s m j", s=4)
+            w1_ps[u] = []
+            for a in range(2):
+                bank = ps_t.tile([P, 2, 512], BF16, name="tp")
+                for s in range(2):
+                    nc.tensor.matmul(
+                        out=bank[:, s, :], lhsT=ident_bf[:], rhs=src[:, 2 * a + s], start=True, stop=True
+                    )
+                w1_ps[u].append(bank)
+
+        def w1_from_psum(u, dst):
+            for a, bank in enumerate(w1_ps[u]):
+                nc.scalar.copy(
+                    out=dst[:, 1024 * a:1024 * (a + 1)].bitcast(F32),
+                    in_=bank[:].rearrange("p s c -> p (s c)").bitcast(F32),
                 )
 
         def pair_quantise(b):
@@ -302,13 +326,22 @@ def tile_moelayer_kernel(tc, x, W1, b1, W2_bytes, W2_scale, b2, temperature, out
         def w2_of(b):
             return plan[b][1] if 0 <= b < beats else None
 
+        def s_slices(b):
+            if b < 0 or w2_of(b + 1) is None:
+                return 0
+            if not w1_of(b):
+                return S_SLICES
+            return PE_SLICES if by_pe(w1_of(b)[-1]) else 0
+
         done_before, y_next, stored = 0, 0, 0
         for b in range(beats):
             w2 = w2_of(b)
             catch_up = len(w1_of(b)) == 2
-            shared = w2 is not None and not w1_of(b - 1) and b > 0
+            for u in w1_of(b + 1):
+                if by_pe(u):
+                    w1_to_psum(u)
             if w2 is not None:
-                w2_widen(w2, "v", range(S_SLICES if shared else 0, 4))
+                w2_widen(w2, "v", range(s_slices(b - 1), 4))
             if catch_up:
                 w1_interleave(w1_of(b)[0], "v", slot(b, w1_cod, w1_of(b)[0]))
             for u in w1_of(b - 4):
@@ -334,10 +367,13 @@ def tile_moelayer_kernel(tc, x, W1, b1, W2_bytes, W2_scale, b2, temperature, out
                 x_turn(0)
             if w2 is not None and b < beats - 1:
                 dst2 = slot(b, w2_cod, w2)
-            if w1_of(b):
-                w1_interleave(w1_of(b)[-1], "s", slot(b, w1_cod, w1_of(b)[-1]))
-            elif w2_of(b + 1) is not None:
-                w2_widen(w2_of(b + 1), "s", range(S_SLICES))
+            for u in w1_of(b)[-1:]:
+                if by_pe(u):
+                    w1_from_psum(u, slot(b, w1_cod, u))
+                else:
+                    w1_interleave(u, "s", slot(b, w1_cod, u))
+            if s_slices(b):
+                w2_widen(w2_of(b + 1), "s", range(s_slices(b)))
             for u in w1_of(b):
                 if u == 1 or u % 8 == 6 and u + 2 < UNITS:
                     x_copy((u + 2) // 8)

@@ -19,8 +19,8 @@ TOK = N // E
 G = H // 512
 UNITS = E * G
 CATCH_UP = (4, 10)
-PE_SLICES = 1
-RUN = 4
+PE_SLICES = 2
+RUN = 2
 AHEAD = 4
 S_SLICES = 3
 PARK = (E - 1) * TOK

@@ -17,12 +17,15 @@ N, D, H, E = 1024, 512, 2048, 8
 P = 128
 TOK = N // E
 G = H // 512
-UNITS = E * G
-CATCH_UP = (4, 10)
-PE_SLICES = 2
+STEPS = E // 2 * G
+CATCH_UP = 3
+PE_STEPS = (6, 8, 10, 12, 14, 15)
+X_BEATS = (4, 8, 10)
 RUN = 2
-AHEAD = 4
-S_SLICES = 3
+AHEAD = 2
+SL_PE = 2
+SL_TAIL = 6
+TAIL_ENG = "vvss"
 PARK = (E - 1) * TOK
 CLAMP_MAX = float(math.log(100.0))
 FLOPS = 2 * N * D * H * 2
@@ -34,21 +37,20 @@ def tile_moelayer_kernel(tc, x, W1, b1, W2_bytes, W2_scale, b2, temperature, out
     with ExitStack() as ctx:
         ctx.enter_context(tc.manual_schedule())
         const = ctx.enter_context(tc.tile_pool(name="const", bufs=1))
-        raw_pool = ctx.enter_context(tc.tile_pool(name="raw_pool", bufs=AHEAD + 4))
+        raw_pool = ctx.enter_context(tc.tile_pool(name="raw_pool", bufs=AHEAD + 3))
         byte_pool = ctx.enter_context(tc.tile_pool(name="byte_pool", bufs=AHEAD + 2))
-        work = ctx.enter_context(tc.tile_pool(name="work", bufs=3))
-        codes = ctx.enter_context(tc.tile_pool(name="codes", bufs=6))
+        work = ctx.enter_context(tc.tile_pool(name="work", bufs=2))
+        codes = ctx.enter_context(tc.tile_pool(name="codes", bufs=3))
         out_pool = ctx.enter_context(tc.tile_pool(name="out_pool", bufs=2))
         ps_t = ctx.enter_context(tc.psum_pool(name="ps_t", bufs=2))
         ps_h = ctx.enter_context(tc.psum_pool(name="ps_h", bufs=4))
         ps_y = ctx.enter_context(tc.psum_pool(name="ps_y", bufs=2))
 
-        w1_raw, w2_raw, b1_col, b2_gain = {}, {}, {}, {}
-        pair, w1_cod, w2_pl, w2_cod = {}, {}, {}, {}
-        h_ps, h_pl, h_grp, h_cod, y_ps, x_grp, x_ps, w1_ps = {}, {}, {}, {}, {}, {}, {}, {}
-
-        def live(u):
-            return 0 <= u < UNITS
+        w1_raw, w1_ps, w1_grp, w1_cod = {}, {}, {}, {}
+        w2_raw, w2_pl, w2_grp, w2_cod = {}, {}, {}, {}
+        h_ps, h_pl, h_grp, h_cod = {}, {}, {}, {}
+        x_rows, x_ps, x_grp, x_cod = {}, {}, {}, {}
+        b1_col, b2_gain, y_ps = {}, {}, {}
 
         def copy(engine, dst, src):
             if engine == "v":
@@ -56,48 +58,45 @@ def tile_moelayer_kernel(tc, x, W1, b1, W2_bytes, W2_scale, b2, temperature, out
             else:
                 nc.scalar.copy(out=dst, in_=src)
 
-        def quantise(name, grp, width):
-            q = codes.tile([P, width], U32, name=name + "_q", align_bytes=64)
-            sc = codes.tile([P, width], U8, name=name + "_s", align_bytes=64)
+        def quantise(name, grp, width, bufs):
+            q = codes.tile([P, width], U32, name=name + "_q", align_bytes=64, bufs=bufs)
+            sc = codes.tile([P, width], U8, name=name + "_s", align_bytes=64, bufs=bufs)
             nc.vector.quantize_mx(out=q[:].bitcast(FP8X4), scales=sc[:], in_=grp)
             return q, sc
 
-        def load_w1(u, parts=1):
-            e, g = divmod(u, G)
-            width = 512 // parts
-            for a in range(parts):
-                raw = raw_pool.tile([P, 4, width], BF16, name="w1_raw", align_bytes=64)
-                c0 = g * 512 + a * width
-                nc.sync.dma_start(
-                    out=raw[:], in_=W1[e].rearrange("(p j) n -> p j n", j=4)[:, :, c0:c0 + width]
-                )
-                w1_raw.setdefault(u, []).append(raw)
+        def load_w1(d, i, cols=slice(0, 512)):
+            k, g = divmod(d, G)
+            if d not in w1_raw:
+                w1_raw[d] = raw_pool.tile([P, 2, 4, 512], BF16, name="w1_raw", align_bytes=64)
+            src = W1[2 * k + i].rearrange("(p j) (g c) -> p g j c", j=4, c=512)[:, g]
+            nc.sync.dma_start(out=w1_raw[d][:, i, :, cols], in_=src[:, :, cols])
 
-        def load_w2(u):
-            e, g = divmod(u, G)
-            wb = byte_pool.tile([P, 2048], U8, name="w2_bytes", align_bytes=64)
-            nc.sync.dma_start(
-                out=wb[:], in_=W2_bytes[e].rearrange("(g p s) n -> p g (s n)", p=P, s=4)[:, g, :]
-            )
-            w2_raw[u] = wb
+        def load_w2(d, i):
+            k, g = divmod(d, G)
+            if d not in w2_raw:
+                w2_raw[d] = byte_pool.tile([P, 4, 2, D], U8, name="w2_bytes", align_bytes=64)
+            src = W2_bytes[2 * k + i].rearrange("(g p s) n -> p g s n", p=P, s=4)[:, g]
+            nc.sync.dma_start(out=w2_raw[d][:, :, i, :], in_=src)
+
+        def load_x(k):
+            x_rows[k] = work.tile([P, 2, D], BF16, name="x_rows", align_bytes=64)
+            src = x.rearrange("(e p) d -> p e d", p=P)
+            nc.sync.dma_start(out=x_rows[k][:], in_=src[:, 2 * k:2 * k + 2, :])
 
         def load_b1(e):
-            col = out_pool.tile([P, G, 16], BF16, name="b1_col", align_bytes=64, bufs=3)
+            col = out_pool.tile([P, G, 16], BF16, name="b1_col", align_bytes=64, bufs=4)
             nc.sync.dma_start(out=col[:, :, 0:4], in_=b1[e].rearrange("(g p s) -> p g s", p=P, s=4))
             b1_col[e] = col
 
         def load_b2(e):
-            row = out_pool.tile([P, D], F32, name="b2_gain", align_bytes=64, bufs=3)
+            row = out_pool.tile([P, D], F32, name="b2_gain", align_bytes=64, bufs=4)
             nc.sync.dma_start(out=row[:], in_=out[PARK + e, :].partition_broadcast(P))
             b2_gain[e] = row
 
         temp = const.tile([P, 1], BF16, name="temp", align_bytes=64)
         scale_head = const.tile([P, 4], F32, name="scale_head", align_bytes=64)
         scale_rest = const.tile([P, G - 1, 8], F32, name="scale_rest", align_bytes=64)
-        x_head = const.tile([P, 2, D], BF16, name="x_head", align_bytes=64)
-        x_rest = const.tile([P, E - 2, D], BF16, name="x_rest", align_bytes=64)
         b2_rows = const.tile([E, D], BF16, name="b2_rows", align_bytes=64)
-        x_src = x.rearrange("(e p) d -> p e d", p=P)
         scale_src = W2_scale.rearrange("o (g p s) z -> p g (o s z)", p=P, s=4)
 
         def w2_scale(g, s):
@@ -105,19 +104,20 @@ def tile_moelayer_kernel(tc, x, W1, b1, W2_bytes, W2_scale, b2, temperature, out
 
         nc.sync.dma_start(out=temp[:], in_=temperature.partition_broadcast(P))
         nc.sync.dma_start(out=scale_head[:], in_=scale_src[:, 0, :])
-        load_w2(0)
-        load_w1(0, parts=2)
-        load_w2(1)
+        load_w2(0, 0)
+        load_w1(0, 0, slice(0, 256))
+        load_w2(0, 1)
+        load_w1(0, 0, slice(256, 512))
+        load_w1(0, 1)
+        load_w2(1, 0)
         nc.sync.dma_start(out=scale_rest[:, :, 0:4], in_=scale_src[:, 1:G, :])
-        load_w1(1)
-        nc.sync.dma_start(out=x_head[:], in_=x_src[:, 0:2, :])
-        load_w2(2)
-        load_w1(2)
-        load_b1(0)
+        load_w2(1, 1)
+        load_w1(1, 0)
+        load_x(0)
+        load_w1(1, 1)
         nc.sync.dma_start(out=b2_rows[:], in_=b2)
-        for u in range(3, AHEAD):
-            load_w2(u)
-            load_w1(u)
+        load_b1(0)
+        load_b1(1)
 
         ident = const.tile([P, P], F32, name="ident", align_bytes=64)
         make_identity(nc, ident[:])
@@ -136,168 +136,150 @@ def tile_moelayer_kernel(tc, x, W1, b1, W2_bytes, W2_scale, b2, temperature, out
             )
             nc.sync.dma_start(out=out[PARK:PARK + E, :], in_=rows[:])
 
-        xq = const.tile([P, E, TOK], U32, name="xq", align_bytes=64)
-        xs = const.tile([P, E, TOK], U8, name="xs", align_bytes=64)
-
         def x_turn(k):
-            tp = ps_t.tile([P, 4, P], F32, name="tp")
+            x_ps[k] = ps_t.tile([P, 4, P], F32, name="tp")
             for i in range(2):
-                rows = x_head[:, i, :] if k == 0 else x_rest[:, 2 * k - 2 + i, :]
-                words = rows.bitcast(F32)
+                words = x_rows[k][:, i, :].bitcast(F32)
                 for u in range(2):
-                    nc.tensor.transpose(tp[:, 2 * i + u, :], words[:, u:256:2], ident[:])
-            x_ps[k] = tp
+                    nc.tensor.transpose(x_ps[k][:, 2 * i + u, :], words[:, u:256:2], ident[:])
 
         def x_copy(k):
-            tp = x_ps[k]
-            xg = work.tile([P, 2, TOK, 4], BF16, name="xg", align_bytes=64, bufs=2)
+            x_grp[k] = work.tile([P, 2, TOK, 4], BF16, name="x_grp", align_bytes=64)
             nc.scalar.copy(
-                out=xg[:].bitcast(F32), in_=tp[:].rearrange("p (i u) r -> p i r u", u=2)
+                out=x_grp[k][:].bitcast(F32), in_=x_ps[k][:].rearrange("p (i u) r -> p i r u", u=2)
             )
-            x_grp[k] = xg
 
         def x_quantise(k):
-            nc.vector.quantize_mx(
-                out=xq[:, 2 * k:2 * k + 2, :].rearrange("p e r -> p (e r)").bitcast(FP8X4),
-                scales=xs[:, 2 * k:2 * k + 2, :].rearrange("p e r -> p (e r)"),
-                in_=x_grp[k][:].rearrange("p e r t -> p (e r t)"),
+            x_cod[k] = quantise("x", x_grp[k][:].rearrange("p e r t -> p (e r t)"), 2 * TOK, 2)
+
+        def w1_tile(d):
+            if d not in w1_grp:
+                w1_grp[d] = work.tile([P, 2, 4, P, 4], BF16, name="w1_grp", align_bytes=64, bufs=3)
+            return w1_grp[d]
+
+        def w1_interleave(d, engine, experts, m=slice(0, P)):
+            copy(
+                engine,
+                w1_tile(d)[:, experts].rearrange("p i s m j -> p i m j s")[:, :, m],
+                w1_raw[d][:, experts].rearrange("p i j (m s) -> p i m j s", s=4)[:, :, m],
             )
 
-        def slot(b, kind, u):
-            if b not in pair:
-                pair[b] = (work.tile([P, 2, 2048], BF16, name="w_grp", align_bytes=64, bufs=4), [])
-            tile, held = pair[b]
-            held.append((kind, u))
-            return tile[:, len(held) - 1, :]
-
-        def w1_interleave(u, engine, dst):
-            grp = dst.rearrange("p (s m j) -> p m j s", s=4, j=4)
-            width = P // len(w1_raw[u])
-            for a, raw in enumerate(w1_raw[u]):
-                copy(
-                    engine,
-                    grp[:, a * width:(a + 1) * width],
-                    raw[:].rearrange("p j (m s) -> p m j s", s=4),
-                )
-
-        def by_pe(u):
-            return u % 4 == 0 and u >= 8
-
-        def w1_to_psum(u):
-            src = w1_raw[u][0][:].rearrange("p j (m s) -> p s m j", s=4)
-            w1_ps[u] = []
+        def w1_to_psum(d):
+            src = w1_raw[d][:, 1].rearrange("p j (m s) -> p s m j", s=4)
+            w1_ps[d] = []
             for a in range(2):
                 bank = ps_t.tile([P, 2, 512], BF16, name="tp")
                 for s in range(2):
                     nc.tensor.matmul(
                         out=bank[:, s, :], lhsT=ident_bf[:], rhs=src[:, 2 * a + s], start=True, stop=True
                     )
-                w1_ps[u].append(bank)
+                w1_ps[d].append(bank)
 
-        def w1_from_psum(u, dst):
-            for a, bank in enumerate(w1_ps[u]):
+        def w1_from_psum(d):
+            dst = w1_tile(d)[:, 1].rearrange("p s m j -> p (s m j)")
+            for a, bank in enumerate(w1_ps[d]):
                 nc.scalar.copy(
                     out=dst[:, 1024 * a:1024 * (a + 1)].bitcast(F32),
                     in_=bank[:].rearrange("p s c -> p (s c)").bitcast(F32),
                 )
 
-        def pair_quantise(b):
-            tile, held = pair[b]
-            q, sc = quantise("w", tile[:, 0:len(held), :].rearrange("p a c -> p (a c)"), 512 * len(held))
-            for a, (kind, u) in enumerate(held):
-                kind[u] = (q[:, 512 * a:512 * (a + 1)], sc[:, 512 * a:512 * (a + 1)])
+        def w1_quantise(d):
+            w1_cod[d] = quantise("w1", w1_grp[d][:].rearrange("p i s m j -> p (i s m j)"), 1024, 2)
 
-        def last_unit(b):
-            u = UNITS - 1
-            tile = slot(b, w2_cod, u).rearrange("p (n s) -> p n s", s=4)
-            for a in range(2):
-                cols = slice(a * 256, (a + 1) * 256)
-                interleave("vs"[a], tile[:, cols, :], w2_pl[u][:, :, cols])
-            h_quantise(u)
-            halves = [
-                quantise("w", tile[:, a * 256:(a + 1) * 256, :].rearrange("p n s -> p (n s)"), 256)
-                for a in range(2)
-            ]
-            for a in range(2):
-                mm2_part(u, a, halves[a][0][:], halves[a][1][:])
-            store(E - 1)
+        def mm1(d):
+            q, sc = w1_cod[d]
+            xq, xs = x_cod[d // G]
+            for i in range(2):
+                ph = ps_h.tile([P, 4, TOK], F32, name="ph")
+                tok = slice(i * TOK, (i + 1) * TOK)
+                for s in range(4):
+                    cols = slice((4 * i + s) * P, (4 * i + s + 1) * P)
+                    nc.tensor.matmul_mx(
+                        out=ph[:, s, :], lhsT=q[:, cols].bitcast(FP8X4), lhsT_scale=sc[:, cols],
+                        rhs=xq[:, tok].bitcast(FP8X4), rhs_scale=xs[:, tok], start=True, stop=True,
+                    )
+                h_ps[d, i] = ph
 
-        def mm1(u):
-            e = u // G
-            q, sc = w1_cod[u]
-            ph = ps_h.tile([P, 4, TOK], F32, name="ph")
-            for s in range(4):
-                nc.tensor.matmul_mx(
-                    out=ph[:, s, :],
-                    lhsT=q[:, s * P:(s + 1) * P].bitcast(FP8X4), lhsT_scale=sc[:, s * P:(s + 1) * P],
-                    rhs=xq[:, e, :].bitcast(FP8X4), rhs_scale=xs[:, e, :],
-                    start=True, stop=True,
-                )
-            h_ps[u] = ph
-
-        def h_relu(u):
-            pl = work.tile([P, 4, TOK], BF16, name="h_pl", align_bytes=64)
-            for s in range(4):
-                nc.scalar.activation(
-                    out=pl[:, s, :], in_=h_ps[u][:, s, :], func=ACT.Relu, bias=b1_col[u // G][:, u % G, s:s + 1]
-                )
-            h_pl[u] = pl
+        def h_relu(d):
+            k, g = divmod(d, G)
+            h_pl[d] = work.tile([P, 4, 2, TOK], BF16, name="h_pl", align_bytes=64, bufs=3)
+            for i in range(2):
+                for s in range(4):
+                    nc.scalar.activation(
+                        out=h_pl[d][:, s, i, :], in_=h_ps[d, i][:, s, :], func=ACT.Relu,
+                        bias=b1_col[2 * k + i][:, g, s:s + 1],
+                    )
 
         def interleave(engine, grp, planes):
             copy(
                 engine,
-                grp.rearrange("p (c i) s -> p c s i", i=RUN),
-                planes.rearrange("p s (c i) -> p c s i", i=RUN),
+                grp.rearrange("p (c r) s -> p c s r", r=RUN),
+                planes.rearrange("p s (c r) -> p c s r", r=RUN),
             )
 
-        def h_interleave(u, engine):
-            grp = work.tile([P, TOK, 4], BF16, name="h_grp", align_bytes=64)
-            interleave(engine, grp[:], h_pl[u][:])
-            h_grp[u] = grp
+        def h_interleave(d, engine):
+            h_grp[d] = work.tile([P, 2 * TOK, 4], BF16, name="h_grp", align_bytes=64, bufs=3)
+            interleave(engine, h_grp[d][:], h_pl[d][:].rearrange("p s i t -> p s (i t)"))
 
-        def h_quantise(u):
-            h_cod[u] = quantise("h", h_grp[u][:].rearrange("p n s -> p (n s)"), TOK)
+        def h_quantise(d):
+            h_cod[d] = quantise("h", h_grp[d][:].rearrange("p n s -> p (n s)"), 2 * TOK, 3)
 
-        def w2_widen(u, engine, slots):
-            g = u % G
-            if u not in w2_pl:
-                w2_pl[u] = work.tile([P, 4, 512], BF16, name="w2_pl", align_bytes=64)
-            pl = w2_pl[u]
+        def w2_widen(d, engine, slots, cols=slice(0, 2 * D)):
+            g = d % G
+            if d not in w2_pl:
+                w2_pl[d] = work.tile([P, 4, 2 * D], BF16, name="w2_pl", align_bytes=64, bufs=3)
             for s in slots:
-                src = w2_raw[u][:, s * 512:(s + 1) * 512].bitcast(FP8)
+                src = w2_raw[d][:, s].rearrange("p i n -> p (i n)")[:, cols].bitcast(FP8)
+                dst = w2_pl[d][:, s, cols]
                 if engine == "v":
                     nc.vector.tensor_scalar(
-                        out=pl[:, s, :], in0=src, scalar1=w2_scale(g, s), scalar2=None,
-                        op0=ALU.mult,
+                        out=dst, in0=src, scalar1=w2_scale(g, s), scalar2=None, op0=ALU.mult
                     )
                 else:
-                    nc.scalar.activation(
-                        out=pl[:, s, :], in_=src, func=ACT.Copy, scale=w2_scale(g, s)
-                    )
+                    nc.scalar.activation(out=dst, in_=src, func=ACT.Copy, scale=w2_scale(g, s))
 
-        def w2_interleave(u, dst):
-            interleave("v", dst.rearrange("p (n s) -> p n s", s=4), w2_pl[u][:])
+        def w2_widen_share(d, engine, halves):
+            whole, odd = divmod(halves, 2)
+            if engine == "s":
+                w2_widen(d, "s", range(whole))
+                if odd:
+                    w2_widen(d, "s", [whole], slice(0, D))
+            else:
+                if odd:
+                    w2_widen(d, "v", [whole], slice(D, 2 * D))
+                w2_widen(d, "v", range(whole + odd, 4))
 
-        def mm2_part(u, a, wq, ws):
-            e, g = divmod(u, G)
-            hq, hs = h_cod[u]
+        def w2_interleave(d, engine="v", cols=slice(0, 2 * D)):
+            if d not in w2_grp:
+                w2_grp[d] = work.tile([P, 2 * D, 4], BF16, name="w2_grp", align_bytes=64)
+            interleave(engine, w2_grp[d][:, cols, :], w2_pl[d][:, :, cols])
+
+        def w2_quantise(d, cols=slice(0, 2 * D)):
+            grp = w2_grp[d][:, cols, :].rearrange("p n s -> p (n s)")
+            return quantise("w2", grp, cols.stop - cols.start, 4)
+
+        def mm2_part(d, i, a, wq, ws):
+            k, g = divmod(d, G)
+            hq, hs = h_cod[d]
+            tok = slice(i * TOK, (i + 1) * TOK)
             nc.tensor.matmul_mx(
-                out=y_ps[e][a][:], lhsT=hq[:].bitcast(FP8X4), lhsT_scale=hs[:],
-                rhs=wq.bitcast(FP8X4), rhs_scale=ws,
-                start=(g == 0), stop=(g == G - 1),
+                out=y_ps[2 * k + i][a][:], lhsT=hq[:, tok].bitcast(FP8X4), lhsT_scale=hs[:, tok],
+                rhs=wq.bitcast(FP8X4), rhs_scale=ws, start=(g == 0), stop=(g == G - 1),
             )
 
-        def mm2(u):
-            e, g = divmod(u, G)
-            if g == 0 and e < E - 1:
-                y_ps[e] = [ps_y.tile([TOK, D], F32, name="py")]
-            if g == 0 and e == E - 1:
-                y_ps[e] = [ps_y.tile([TOK, 256], F32, name="py"), ps_t.tile([TOK, 256], F32, name="tp")]
-            wq, ws = w2_cod[u]
-            width = D // len(y_ps[e])
-            for a in range(len(y_ps[e])):
-                cols = slice(a * width, (a + 1) * width)
-                mm2_part(u, a, wq[:, cols], ws[:, cols])
+        def mm2(d):
+            k, g = divmod(d, G)
+            wq, ws = w2_cod[d]
+            for i in range(2):
+                e = 2 * k + i
+                if g == 0 and e < E - 1:
+                    y_ps[e] = [ps_y.tile([TOK, D], F32, name="py")]
+                if g == 0 and e == E - 1:
+                    y_ps[e] = [ps_y.tile([TOK, 256], F32, name="py"), ps_h.tile([TOK, 256], F32, name="ph")]
+                width = D // len(y_ps[e])
+                for a in range(len(y_ps[e])):
+                    cols = slice(i * D + a * width, i * D + (a + 1) * width)
+                    mm2_part(d, i, a, wq[:, cols], ws[:, cols])
 
         def store(e):
             width = D // len(y_ps[e])
@@ -310,95 +292,117 @@ def tile_moelayer_kernel(tc, x, W1, b1, W2_bytes, W2_scale, b2, temperature, out
                 )
                 nc.sync.dma_start(out=out[e * TOK:(e + 1) * TOK, cols], in_=y[:])
 
-        plan, u1, u2 = [], 0, 0
-        while u2 < UNITS:
-            if len(plan) in CATCH_UP:
-                plan.append(([u1, u1 + 1], None))
-                u1 += 2
-            else:
-                plan.append(([u1] if u1 < UNITS else [], u2))
-                u1, u2 = min(u1 + 1, UNITS), u2 + 1
-        beats = len(plan)
+        beats = STEPS + 1
 
         def w1_of(b):
-            return plan[b][0] if 0 <= b < beats else []
+            if b == CATCH_UP:
+                return [b, b + 1]
+            d = b if b < CATCH_UP else b + 1
+            return [d] if 0 <= d < STEPS else []
 
         def w2_of(b):
-            return plan[b][1] if 0 <= b < beats else None
+            if b == CATCH_UP or not 0 <= b < beats:
+                return []
+            return [b if b < CATCH_UP else b - 1]
 
         def s_slices(b):
-            if b < 0 or w2_of(b + 1) is None:
+            if b < 0 or not w2_of(b + 1):
                 return 0
             if not w1_of(b):
-                return S_SLICES
-            return PE_SLICES if by_pe(w1_of(b)[-1]) else 0
+                return SL_TAIL
+            return SL_PE if w1_of(b)[-1] in PE_STEPS else 0
 
-        done_before, y_next, stored = 0, 0, 0
+        first, second = slice(0, D), slice(D, 2 * D)
+        y_next, stored = 0, 0
         for b in range(beats):
-            w2 = w2_of(b)
-            catch_up = len(w1_of(b)) == 2
-            for u in w1_of(b + 1):
-                if by_pe(u):
-                    w1_to_psum(u)
-            if w2 is not None:
-                w2_widen(w2, "v", range(s_slices(b - 1), 4))
-            if catch_up:
-                w1_interleave(w1_of(b)[0], "v", slot(b, w1_cod, w1_of(b)[0]))
-            for u in w1_of(b - 4):
-                if u < UNITS - 1:
-                    h_quantise(u)
-            for u in w1_of(b - 1):
-                if u == 1 or u % 8 == 7 and u + 1 < UNITS:
-                    x_quantise((u + 1) // 8)
-            if b - 1 in pair:
-                pair_quantise(b - 1)
-            if b == 2:
-                mm1(0)
-            for u in w1_of(b - 1):
-                if u > 0:
-                    mm1(u)
-            while y_next in h_cod and y_next in w2_cod:
-                mm2(y_next)
-                y_next += 1
-            for u in w1_of(b + 1):
-                if u % 8 == 6 and u + 2 < UNITS:
-                    x_turn((u + 2) // 8)
-            if b == 1:
-                x_turn(0)
-            if w2 is not None and b < beats - 1:
-                dst2 = slot(b, w2_cod, w2)
-            for u in w1_of(b)[-1:]:
-                if by_pe(u):
-                    w1_from_psum(u, slot(b, w1_cod, u))
-                else:
-                    w1_interleave(u, "s", slot(b, w1_cod, u))
-            if s_slices(b):
-                w2_widen(w2_of(b + 1), "s", range(s_slices(b)))
-            for u in w1_of(b):
-                if u == 1 or u % 8 == 6 and u + 2 < UNITS:
-                    x_copy((u + 2) // 8)
-            for u in w1_of(b - 3):
-                h_interleave(u, "v" if catch_up else "s")
-            for u in w1_of(b - 2):
-                h_relu(u)
-            if w2 is not None and b < beats - 1:
-                w2_interleave(w2, dst2)
+            last = b == beats - 1
+            for d in w1_of(b):
+                if d in PE_STEPS:
+                    w1_from_psum(d)
+            if b + 1 in X_BEATS:
+                x_turn(X_BEATS.index(b + 1) + 1)
+            if b == 0:
+                w2_widen(0, "v", range(4), first)
+                w2_widen(0, "v", range(4), second)
+            else:
+                for d in w2_of(b):
+                    w2_widen_share(d, "v", s_slices(b - 1))
             if b == 2:
                 park_b2()
-            if stored < done_before:
+            if b == CATCH_UP:
+                w1_interleave(b, "v", slice(0, 2))
+            while stored < 2 * (y_next // G):
                 store(stored)
                 stored += 1
-            done_before = y_next // G
-            if w2_of(b + AHEAD) is not None:
-                load_w2(w2_of(b + AHEAD))
-            for u in w1_of(b + AHEAD):
-                load_w1(u)
-                if u % G == 0:
-                    load_b1(u // G)
-            if b == 3:
-                load_b2(0)
-            if b % G == 1 and 0 < b // G < E:
-                load_b2(b // G)
+            if b == 1:
+                x_turn(0)
+                w1_interleave(1, "s", slice(0, 1))
+                x_copy(0)
+                w2_cod[0] = w2_quantise(0)
+                w1_quantise(0)
+                x_quantise(0)
+                mm1(0)
+            for d in w1_of(b - 3):
+                h_quantise(d)
+            if b in X_BEATS:
+                x_quantise(X_BEATS.index(b) + 1)
+            if b > 1:
+                for d in w1_of(b - 1):
+                    w1_quantise(d)
+                    mm1(d)
+                for d in w2_of(b - 1):
+                    w2_cod[d] = w2_quantise(d)
             if b == 0:
-                nc.sync.dma_start(out=x_rest[:], in_=x_src[:, 2:E, :])
-        last_unit(beats - 1)
+                w1_interleave(0, "s", slice(0, 1), slice(0, 64))
+                w1_interleave(0, "s", slice(0, 1), slice(64, P))
+                w1_interleave(0, "s", slice(1, 2))
+            for d in w1_of(b)[-1:]:
+                if d in PE_STEPS:
+                    w1_interleave(d, "s", slice(0, 1))
+                elif b > 0:
+                    w1_interleave(d, "s", slice(1 if b == 1 else 0, 2))
+            for d in w1_of(b + 1):
+                if d in PE_STEPS:
+                    w1_to_psum(d)
+            for d in w1_of(b - 2):
+                h_interleave(d, "v" if b == CATCH_UP else "s")
+            if s_slices(b):
+                w2_widen_share(w2_of(b + 1)[0], "s", s_slices(b))
+            if b + 1 in X_BEATS:
+                x_copy(X_BEATS.index(b + 1) + 1)
+            for d in w1_of(b - 1):
+                h_relu(d)
+            if b == 0:
+                w2_interleave(0, "v", first)
+                w2_interleave(0, "v", second)
+            elif not last:
+                for d in w2_of(b):
+                    w2_interleave(d)
+            while y_next in h_cod and y_next in w2_cod and y_next // G < stored // 2 + 1:
+                mm2(y_next)
+                y_next += 1
+            for i in range(2):
+                for d in w2_of(b + AHEAD):
+                    load_w2(d, i)
+                for d in w1_of(b + AHEAD):
+                    load_w1(d, i)
+                    if d % G == 0:
+                        load_b1(d // 2 + i)
+            if b + 3 in X_BEATS:
+                load_x(X_BEATS.index(b + 3) + 1)
+            if b % G == 3:
+                load_b2(2 * (b // G))
+                load_b2(2 * (b // G) + 1)
+
+        d = STEPS - 1
+        quarters = [slice(256 * a, 256 * (a + 1)) for a in range(4)]
+        for a in range(4):
+            w2_interleave(d, TAIL_ENG[a], quarters[a])
+        h_quantise(d)
+        wq, ws = w2_quantise(d, first)
+        mm2_part(d, 0, 0, wq[:], ws[:])
+        halves = [w2_quantise(d, cols) for cols in quarters[2:]]
+        store(E - 2)
+        for a in range(2):
+            mm2_part(d, 1, a, halves[a][0][:], halves[a][1][:])
+        store(E - 1)

@@ -17,14 +17,17 @@ N, D, H, E = 1024, 512, 2048, 8
 P = 128
 TOK = N // E
 G = H // 512
-STEPS = E // 2 * G
-CATCH_UP = 3
-PE_STEPS = (6, 8, 10, 12, 14, 15)
-X_BEATS = (4, 8, 10)
+PAIRS = E // 2
+STEPS = PAIRS * G
+COLS = 2 * D
+PE_STEPS = (6, 7, 10, 11, 14, 15)
 RUN = 2
-AHEAD = 2
-SL_PE = 2
-SL_TAIL = 6
+AHEAD = 3
+POOL_FIRST = 704
+POOL_COLS = 896
+V_COLS_HEAD = 896
+V_COLS = 512
+V_COLS_TAIL = 512
 TAIL_ENG = "vvss"
 PARK = (E - 1) * TOK
 CLAMP_MAX = float(math.log(100.0))
@@ -37,10 +40,9 @@ def tile_moelayer_kernel(tc, x, W1, b1, W2_bytes, W2_scale, b2, temperature, out
     with ExitStack() as ctx:
         ctx.enter_context(tc.manual_schedule())
         const = ctx.enter_context(tc.tile_pool(name="const", bufs=1))
-        raw_pool = ctx.enter_context(tc.tile_pool(name="raw_pool", bufs=AHEAD + 3))
-        byte_pool = ctx.enter_context(tc.tile_pool(name="byte_pool", bufs=AHEAD + 2))
+        raw_pool = ctx.enter_context(tc.tile_pool(name="raw_pool", bufs=AHEAD + 1))
         work = ctx.enter_context(tc.tile_pool(name="work", bufs=2))
-        codes = ctx.enter_context(tc.tile_pool(name="codes", bufs=3))
+        codes = ctx.enter_context(tc.tile_pool(name="codes", bufs=2))
         out_pool = ctx.enter_context(tc.tile_pool(name="out_pool", bufs=2))
         ps_t = ctx.enter_context(tc.psum_pool(name="ps_t", bufs=2))
         ps_h = ctx.enter_context(tc.psum_pool(name="ps_h", bufs=4))
@@ -48,7 +50,7 @@ def tile_moelayer_kernel(tc, x, W1, b1, W2_bytes, W2_scale, b2, temperature, out
 
         w1_raw, w1_ps, w1_grp, w1_cod = {}, {}, {}, {}
         w2_raw, w2_pl, w2_grp, w2_cod = {}, {}, {}, {}
-        h_ps, h_pl, h_grp, h_cod = {}, {}, {}, {}
+        h_ps, h_grp, h_cod = {}, {}, {}
         x_rows, x_ps, x_grp, x_cod = {}, {}, {}, {}
         b1_col, b2_gain, y_ps = {}, {}, {}
 
@@ -64,34 +66,46 @@ def tile_moelayer_kernel(tc, x, W1, b1, W2_bytes, W2_scale, b2, temperature, out
             nc.vector.quantize_mx(out=q[:].bitcast(FP8X4), scales=sc[:], in_=grp)
             return q, sc
 
-        def load_w1(d, i, cols=slice(0, 512)):
+        def load_w1_part(d, i, cols=slice(0, 512)):
             k, g = divmod(d, G)
             if d not in w1_raw:
                 w1_raw[d] = raw_pool.tile([P, 2, 4, 512], BF16, name="w1_raw", align_bytes=64)
             src = W1[2 * k + i].rearrange("(p j) (g c) -> p g j c", j=4, c=512)[:, g]
             nc.sync.dma_start(out=w1_raw[d][:, i, :, cols], in_=src[:, :, cols])
 
-        def load_w2(d, i):
-            k, g = divmod(d, G)
-            if d not in w2_raw:
-                w2_raw[d] = byte_pool.tile([P, 4, 2, D], U8, name="w2_bytes", align_bytes=64)
+        def load_w2_part(j, i):
+            k, g = divmod(j, G)
+            if j not in w2_raw:
+                w2_raw[j] = raw_pool.tile([P, 4, 2, D], U8, name="w2_bytes", align_bytes=64)
             src = W2_bytes[2 * k + i].rearrange("(g p s) n -> p g s n", p=P, s=4)[:, g]
-            nc.sync.dma_start(out=w2_raw[d][:, :, i, :], in_=src)
+            nc.sync.dma_start(out=w2_raw[j][:, :, i, :], in_=src)
+
+        def load_w1(d):
+            if d < STEPS:
+                load_w1_part(d, 0)
+                load_w1_part(d, 1)
+
+        def load_w2(j):
+            if j < STEPS:
+                load_w2_part(j, 0)
+                load_w2_part(j, 1)
 
         def load_x(k):
             x_rows[k] = work.tile([P, 2, D], BF16, name="x_rows", align_bytes=64)
             src = x.rearrange("(e p) d -> p e d", p=P)
             nc.sync.dma_start(out=x_rows[k][:], in_=src[:, 2 * k:2 * k + 2, :])
 
-        def load_b1(e):
-            col = out_pool.tile([P, G, 16], BF16, name="b1_col", align_bytes=64, bufs=4)
-            nc.sync.dma_start(out=col[:, :, 0:4], in_=b1[e].rearrange("(g p s) -> p g s", p=P, s=4))
-            b1_col[e] = col
+        def load_b1(k):
+            for e in (2 * k, 2 * k + 1):
+                b1_col[e] = out_pool.tile([P, G, 16], BF16, name="b1_col", align_bytes=64, bufs=4)
+                nc.sync.dma_start(
+                    out=b1_col[e][:, :, 0:4], in_=b1[e].rearrange("(g p s) -> p g s", p=P, s=4)
+                )
 
-        def load_b2(e):
-            row = out_pool.tile([P, D], F32, name="b2_gain", align_bytes=64, bufs=4)
-            nc.sync.dma_start(out=row[:], in_=out[PARK + e, :].partition_broadcast(P))
-            b2_gain[e] = row
+        def load_b2(k):
+            for e in (2 * k, 2 * k + 1):
+                b2_gain[e] = out_pool.tile([P, D], F32, name="b2_gain", align_bytes=64)
+                nc.sync.dma_start(out=b2_gain[e][:], in_=out[PARK + e, :].partition_broadcast(P))
 
         temp = const.tile([P, 1], BF16, name="temp", align_bytes=64)
         scale_head = const.tile([P, 4], F32, name="scale_head", align_bytes=64)
@@ -104,20 +118,21 @@ def tile_moelayer_kernel(tc, x, W1, b1, W2_bytes, W2_scale, b2, temperature, out
 
         nc.sync.dma_start(out=temp[:], in_=temperature.partition_broadcast(P))
         nc.sync.dma_start(out=scale_head[:], in_=scale_src[:, 0, :])
-        load_w2(0, 0)
-        load_w1(0, 0, slice(0, 256))
-        load_w2(0, 1)
-        load_w1(0, 0, slice(256, 512))
-        load_w1(0, 1)
-        load_w2(1, 0)
+        load_w2_part(0, 0)
+        load_w1_part(0, 0, slice(0, 256))
+        load_w2_part(0, 1)
+        load_w1_part(0, 0, slice(256, 512))
+        load_w1_part(0, 1)
+        load_w2_part(1, 0)
         nc.sync.dma_start(out=scale_rest[:, :, 0:4], in_=scale_src[:, 1:G, :])
-        load_w2(1, 1)
-        load_w1(1, 0)
+        load_w2_part(1, 1)
+        load_w1_part(1, 0)
         load_x(0)
-        load_w1(1, 1)
+        load_w1_part(1, 1)
+        load_w2(2)
+        load_w1(2)
         nc.sync.dma_start(out=b2_rows[:], in_=b2)
         load_b1(0)
-        load_b1(1)
 
         ident = const.tile([P, P], F32, name="ident", align_bytes=64)
         make_identity(nc, ident[:])
@@ -144,7 +159,7 @@ def tile_moelayer_kernel(tc, x, W1, b1, W2_bytes, W2_scale, b2, temperature, out
                     nc.tensor.transpose(x_ps[k][:, 2 * i + u, :], words[:, u:256:2], ident[:])
 
         def x_copy(k):
-            x_grp[k] = work.tile([P, 2, TOK, 4], BF16, name="x_grp", align_bytes=64)
+            x_grp[k] = work.tile([P, 2, TOK, 4], BF16, name="x_grp", align_bytes=64, bufs=1)
             nc.scalar.copy(
                 out=x_grp[k][:].bitcast(F32), in_=x_ps[k][:].rearrange("p (i u) r -> p i r u", u=2)
             )
@@ -157,14 +172,15 @@ def tile_moelayer_kernel(tc, x, W1, b1, W2_bytes, W2_scale, b2, temperature, out
                 w1_grp[d] = work.tile([P, 2, 4, P, 4], BF16, name="w1_grp", align_bytes=64, bufs=3)
             return w1_grp[d]
 
-        def w1_interleave(d, engine, experts, m=slice(0, P)):
-            copy(
-                engine,
-                w1_tile(d)[:, experts].rearrange("p i s m j -> p i m j s")[:, :, m],
-                w1_raw[d][:, experts].rearrange("p i j (m s) -> p i m j s", s=4)[:, :, m],
+        def w1_copy(d, experts, m=slice(0, P)):
+            nc.scalar.copy(
+                out=w1_tile(d)[:, experts].rearrange("p i s m j -> p i m j s")[:, :, m],
+                in_=w1_raw[d][:, experts].rearrange("p i j (m s) -> p i m j s", s=4)[:, :, m],
             )
 
         def w1_to_psum(d):
+            if d not in PE_STEPS:
+                return
             src = w1_raw[d][:, 1].rearrange("p j (m s) -> p s m j", s=4)
             w1_ps[d] = []
             for a in range(2):
@@ -175,16 +191,23 @@ def tile_moelayer_kernel(tc, x, W1, b1, W2_bytes, W2_scale, b2, temperature, out
                     )
                 w1_ps[d].append(bank)
 
-        def w1_from_psum(d):
-            dst = w1_tile(d)[:, 1].rearrange("p s m j -> p (s m j)")
-            for a, bank in enumerate(w1_ps[d]):
-                nc.scalar.copy(
-                    out=dst[:, 1024 * a:1024 * (a + 1)].bitcast(F32),
-                    in_=bank[:].rearrange("p s c -> p (s c)").bitcast(F32),
-                )
+        def w1_interleave(d):
+            if d >= STEPS:
+                return
+            if d in PE_STEPS:
+                w1_copy(d, slice(0, 1))
+                dst = w1_tile(d)[:, 1].rearrange("p s m j -> p (s m j)")
+                for a, bank in enumerate(w1_ps[d]):
+                    nc.scalar.copy(
+                        out=dst[:, 1024 * a:1024 * (a + 1)].bitcast(F32),
+                        in_=bank[:].rearrange("p s c -> p (s c)").bitcast(F32),
+                    )
+            else:
+                w1_copy(d, slice(0, 2))
+            load_w1(d + AHEAD)
 
         def w1_quantise(d):
-            w1_cod[d] = quantise("w1", w1_grp[d][:].rearrange("p i s m j -> p (i s m j)"), 1024, 2)
+            w1_cod[d] = quantise("w1", w1_grp[d][:].rearrange("p i s m j -> p (i s m j)"), 1024, G)
 
         def mm1(d):
             q, sc = w1_cod[d]
@@ -200,76 +223,78 @@ def tile_moelayer_kernel(tc, x, W1, b1, W2_bytes, W2_scale, b2, temperature, out
                     )
                 h_ps[d, i] = ph
 
-        def h_relu(d):
+        def h_bias(d):
             k, g = divmod(d, G)
-            h_pl[d] = work.tile([P, 4, 2, TOK], BF16, name="h_pl", align_bytes=64, bufs=3)
+            if k not in h_grp:
+                h_grp[k] = work.tile([P, G, 2, TOK, 4], BF16, name="h_grp", align_bytes=64, bufs=1)
             for i in range(2):
-                for s in range(4):
-                    nc.scalar.activation(
-                        out=h_pl[d][:, s, i, :], in_=h_ps[d, i][:, s, :], func=ACT.Relu,
-                        bias=b1_col[2 * k + i][:, g, s:s + 1],
-                    )
+                bias = b1_col[2 * k + i][:, g, 0:4].unsqueeze(1).unsqueeze(3)
+                nc.vector.tensor_tensor(
+                    out=h_grp[k][:, g, i].rearrange("p (c r) s -> p c s r", r=RUN),
+                    in0=h_ps[d, i][:].rearrange("p s (c r) -> p c s r", r=RUN),
+                    in1=bias.to_broadcast([P, TOK // RUN, 4, RUN]), op=ALU.add,
+                )
 
-        def interleave(engine, grp, planes):
-            copy(
-                engine,
-                grp.rearrange("p (c r) s -> p c s r", r=RUN),
-                planes.rearrange("p s (c r) -> p c s r", r=RUN),
-            )
+        def h_relu(k):
+            flat = h_grp[k][:].rearrange("p g i t s -> p (g i t s)")
+            nc.vector.tensor_scalar_max(flat, flat, 0.0)
 
-        def h_interleave(d, engine):
-            h_grp[d] = work.tile([P, 2 * TOK, 4], BF16, name="h_grp", align_bytes=64, bufs=3)
-            interleave(engine, h_grp[d][:], h_pl[d][:].rearrange("p s i t -> p s (i t)"))
+        def h_quantise(k):
+            h_cod[k] = quantise("h", h_grp[k][:].rearrange("p g i t s -> p (g i t s)"), G * 2 * TOK, 2)
 
-        def h_quantise(d):
-            h_cod[d] = quantise("h", h_grp[d][:].rearrange("p n s -> p (n s)"), 2 * TOK, 3)
-
-        def w2_widen(d, engine, slots, cols=slice(0, 2 * D)):
-            g = d % G
-            if d not in w2_pl:
-                w2_pl[d] = work.tile([P, 4, 2 * D], BF16, name="w2_pl", align_bytes=64, bufs=3)
-            for s in slots:
-                src = w2_raw[d][:, s].rearrange("p i n -> p (i n)")[:, cols].bitcast(FP8)
-                dst = w2_pl[d][:, s, cols]
+        def w2_widen(j, engine, cols=slice(0, COLS)):
+            if j not in w2_pl:
+                w2_pl[j] = work.tile([P, 4, COLS], BF16, name="w2_pl", align_bytes=64, bufs=3)
+            for s in range(4):
+                src = w2_raw[j][:, s].rearrange("p i n -> p (i n)")[:, cols].bitcast(FP8)
+                dst = w2_pl[j][:, s, cols]
                 if engine == "v":
                     nc.vector.tensor_scalar(
-                        out=dst, in0=src, scalar1=w2_scale(g, s), scalar2=None, op0=ALU.mult
+                        out=dst, in0=src, scalar1=w2_scale(j % G, s), scalar2=None, op0=ALU.mult
                     )
                 else:
-                    nc.scalar.activation(out=dst, in_=src, func=ACT.Copy, scale=w2_scale(g, s))
+                    nc.scalar.activation(out=dst, in_=src, func=ACT.Copy, scale=w2_scale(j % G, s))
+            if cols.stop == COLS:
+                load_w2(j + AHEAD)
 
-        def w2_widen_share(d, engine, halves):
-            whole, odd = divmod(halves, 2)
-            if engine == "s":
-                w2_widen(d, "s", range(whole))
-                if odd:
-                    w2_widen(d, "s", [whole], slice(0, D))
-            else:
-                if odd:
-                    w2_widen(d, "v", [whole], slice(D, 2 * D))
-                w2_widen(d, "v", range(whole + odd, 4))
+        def w2_tile(j):
+            if j not in w2_grp:
+                w2_grp[j] = work.tile([P, COLS, 4], BF16, name="w2_grp", align_bytes=64, bufs=3)
+            return w2_grp[j]
 
-        def w2_interleave(d, engine="v", cols=slice(0, 2 * D)):
-            if d not in w2_grp:
-                w2_grp[d] = work.tile([P, 2 * D, 4], BF16, name="w2_grp", align_bytes=64)
-            interleave(engine, w2_grp[d][:, cols, :], w2_pl[d][:, :, cols])
+        def w2_interleave(j, engine, cols=slice(0, COLS)):
+            if cols.start < cols.stop:
+                copy(
+                    engine,
+                    w2_tile(j)[:, cols, :].rearrange("p (c r) s -> p c s r", r=RUN),
+                    w2_pl[j][:, :, cols].rearrange("p s (c r) -> p c s r", r=RUN),
+                )
 
-        def w2_quantise(d, cols=slice(0, 2 * D)):
-            grp = w2_grp[d][:, cols, :].rearrange("p n s -> p (n s)")
+        def w2_interleave_pool(j, cols):
+            nc.gpsimd.tensor_scalar(
+                out=w2_tile(j)[:, cols, :], in0=w2_pl[j][:, :, cols].rearrange("p s c -> p c s"),
+                scalar1=1.0, scalar2=0.0, op0=ALU.mult, op1=ALU.add,
+            )
+
+        def w2_quantise_part(j, cols):
+            grp = w2_grp[j][:, cols, :].rearrange("p n s -> p (n s)")
             return quantise("w2", grp, cols.stop - cols.start, 4)
 
-        def mm2_part(d, i, a, wq, ws):
-            k, g = divmod(d, G)
-            hq, hs = h_cod[d]
-            tok = slice(i * TOK, (i + 1) * TOK)
+        def w2_quantise(j):
+            w2_cod[j] = w2_quantise_part(j, slice(0, COLS))
+
+        def mm2_part(j, i, a, wq, ws):
+            k, g = divmod(j, G)
+            hq, hs = h_cod[k]
+            tok = slice((2 * g + i) * TOK, (2 * g + i + 1) * TOK)
             nc.tensor.matmul_mx(
                 out=y_ps[2 * k + i][a][:], lhsT=hq[:, tok].bitcast(FP8X4), lhsT_scale=hs[:, tok],
                 rhs=wq.bitcast(FP8X4), rhs_scale=ws, start=(g == 0), stop=(g == G - 1),
             )
 
-        def mm2(d):
-            k, g = divmod(d, G)
-            wq, ws = w2_cod[d]
+        def mm2(j):
+            k, g = divmod(j, G)
+            wq, ws = w2_cod[j]
             for i in range(2):
                 e = 2 * k + i
                 if g == 0 and e < E - 1:
@@ -279,7 +304,7 @@ def tile_moelayer_kernel(tc, x, W1, b1, W2_bytes, W2_scale, b2, temperature, out
                 width = D // len(y_ps[e])
                 for a in range(len(y_ps[e])):
                     cols = slice(i * D + a * width, i * D + (a + 1) * width)
-                    mm2_part(d, i, a, wq[:, cols], ws[:, cols])
+                    mm2_part(j, i, a, wq[:, cols], ws[:, cols])
 
         def store(e):
             width = D // len(y_ps[e])
@@ -292,117 +317,123 @@ def tile_moelayer_kernel(tc, x, W1, b1, W2_bytes, W2_scale, b2, temperature, out
                 )
                 nc.sync.dma_start(out=out[e * TOK:(e + 1) * TOK, cols], in_=y[:])
 
-        beats = STEPS + 1
+        def window(k):
+            d, j = G * k, 3 * k + 3
+            pool_cols = POOL_FIRST if k == 0 else POOL_COLS
+            w2_widen(j, "v")
+            w2_interleave_pool(j, slice(0, pool_cols))
+            w2_interleave(j, "s", slice(pool_cols, COLS))
+            h_bias(d)
+            mm1(d + 2)
+            h_bias(d + 1)
+            mm1(d + 3)
+            h_bias(d + 2)
+            h_bias(d + 3)
+            if k > 0:
+                store(2 * k - 2)
+                store(2 * k - 1)
+            load_b2(k)
+            h_relu(k)
 
-        def w1_of(b):
-            if b == CATCH_UP:
-                return [b, b + 1]
-            d = b if b < CATCH_UP else b + 1
-            return [d] if 0 <= d < STEPS else []
+        first, second = slice(0, D), slice(D, COLS)
+        w2_widen(0, "v", first)
+        w2_widen(0, "v", second)
+        w1_copy(0, slice(0, 1), slice(0, 64))
+        w1_copy(0, slice(0, 1), slice(64, P))
+        w1_copy(0, slice(1, 2))
+        load_w1(AHEAD)
+        w2_interleave(0, "v", first)
+        w2_interleave(0, "v", second)
+        w2_widen(1, "v")
+        w2_quantise(0)
+        w1_quantise(0)
+        x_turn(0)
+        w1_copy(1, slice(0, 1))
+        w1_copy(1, slice(1, 2))
+        load_w1(1 + AHEAD)
+        x_copy(0)
+        w2_interleave(1, "v")
+        w2_widen(2, "v")
+        w2_quantise(1)
+        w1_quantise(1)
+        park_b2()
+        x_quantise(0)
+        mm1(0)
+        mm1(1)
+        w1_interleave(2)
+        w2_interleave(2, "v", slice(0, V_COLS_HEAD))
+        w2_interleave(2, "s", slice(V_COLS_HEAD, COLS))
+        w1_quantise(2)
+        w1_interleave(3)
+        load_x(1)
+        load_b1(1)
+        w2_quantise(2)
+        w1_quantise(3)
+        w1_interleave(4)
+        window(0)
 
-        def w2_of(b):
-            if b == CATCH_UP or not 0 <= b < beats:
-                return []
-            return [b if b < CATCH_UP else b - 1]
+        for k in range(1, PAIRS):
+            d, j = G * k, 3 * k
+            w1_interleave(d + 1)
+            w1_to_psum(d + 2)
+            w2_widen(j + 1, "v")
+            h_quantise(k - 1)
+            for ready in range(d - G, j):
+                mm2(ready)
+            w1_interleave(d + 2)
+            x_turn(k)
+            w2_quantise(j)
+            if j < d:
+                mm2(j)
+            w1_quantise(d)
+            w2_interleave(j + 1, "s")
+            x_copy(k)
+            w1_to_psum(d + 3)
+            w2_widen(j + 2, "v")
+            w1_quantise(d + 1)
+            x_quantise(k)
+            w1_quantise(d + 2)
+            mm1(d)
+            mm1(d + 1)
+            w1_interleave(d + 3)
+            w1_to_psum(d + 4)
+            w2_quantise(j + 1)
+            if j + 1 < d:
+                mm2(j + 1)
+            w2_interleave(j + 2, "v", slice(0, V_COLS))
+            w2_interleave(j + 2, "s", slice(V_COLS, COLS))
+            w1_quantise(d + 3)
+            if k + 1 < PAIRS:
+                load_x(k + 1)
+                load_b1(k + 1)
+            w2_quantise(j + 2)
+            if j + 2 < d:
+                mm2(j + 2)
+            w1_interleave(d + 4)
+            if k == PAIRS - 1:
+                w2_widen(STEPS - 3, "s")
+            window(k)
 
-        def s_slices(b):
-            if b < 0 or not w2_of(b + 1):
-                return 0
-            if not w1_of(b):
-                return SL_TAIL
-            return SL_PE if w1_of(b)[-1] in PE_STEPS else 0
-
-        first, second = slice(0, D), slice(D, 2 * D)
-        y_next, stored = 0, 0
-        for b in range(beats):
-            last = b == beats - 1
-            for d in w1_of(b):
-                if d in PE_STEPS:
-                    w1_from_psum(d)
-            if b + 1 in X_BEATS:
-                x_turn(X_BEATS.index(b + 1) + 1)
-            if b == 0:
-                w2_widen(0, "v", range(4), first)
-                w2_widen(0, "v", range(4), second)
-            else:
-                for d in w2_of(b):
-                    w2_widen_share(d, "v", s_slices(b - 1))
-            if b == 2:
-                park_b2()
-            if b == CATCH_UP:
-                w1_interleave(b, "v", slice(0, 2))
-            while stored < 2 * (y_next // G):
-                store(stored)
-                stored += 1
-            if b == 1:
-                x_turn(0)
-                w1_interleave(1, "s", slice(0, 1))
-                x_copy(0)
-                w2_cod[0] = w2_quantise(0)
-                w1_quantise(0)
-                x_quantise(0)
-                mm1(0)
-            for d in w1_of(b - 3):
-                h_quantise(d)
-            if b in X_BEATS:
-                x_quantise(X_BEATS.index(b) + 1)
-            if b > 1:
-                for d in w1_of(b - 1):
-                    w1_quantise(d)
-                    mm1(d)
-                for d in w2_of(b - 1):
-                    w2_cod[d] = w2_quantise(d)
-            if b == 0:
-                w1_interleave(0, "s", slice(0, 1), slice(0, 64))
-                w1_interleave(0, "s", slice(0, 1), slice(64, P))
-                w1_interleave(0, "s", slice(1, 2))
-            for d in w1_of(b)[-1:]:
-                if d in PE_STEPS:
-                    w1_interleave(d, "s", slice(0, 1))
-                elif b > 0:
-                    w1_interleave(d, "s", slice(1 if b == 1 else 0, 2))
-            for d in w1_of(b + 1):
-                if d in PE_STEPS:
-                    w1_to_psum(d)
-            for d in w1_of(b - 2):
-                h_interleave(d, "v" if b == CATCH_UP else "s")
-            if s_slices(b):
-                w2_widen_share(w2_of(b + 1)[0], "s", s_slices(b))
-            if b + 1 in X_BEATS:
-                x_copy(X_BEATS.index(b + 1) + 1)
-            for d in w1_of(b - 1):
-                h_relu(d)
-            if b == 0:
-                w2_interleave(0, "v", first)
-                w2_interleave(0, "v", second)
-            elif not last:
-                for d in w2_of(b):
-                    w2_interleave(d)
-            while y_next in h_cod and y_next in w2_cod and y_next // G < stored // 2 + 1:
-                mm2(y_next)
-                y_next += 1
-            for i in range(2):
-                for d in w2_of(b + AHEAD):
-                    load_w2(d, i)
-                for d in w1_of(b + AHEAD):
-                    load_w1(d, i)
-                    if d % G == 0:
-                        load_b1(d // 2 + i)
-            if b + 3 in X_BEATS:
-                load_x(X_BEATS.index(b + 3) + 1)
-            if b % G == 3:
-                load_b2(2 * (b // G))
-                load_b2(2 * (b // G) + 1)
-
-        d = STEPS - 1
+        j = STEPS - 4
+        w2_widen(j + 2, "s")
+        w2_widen(j + 3, "v")
+        h_quantise(PAIRS - 1)
+        w2_quantise(j)
+        mm2(j)
+        w2_interleave(j + 1, "s")
+        w2_interleave(j + 2, "v", slice(0, V_COLS_TAIL))
+        w2_interleave(j + 2, "s", slice(V_COLS_TAIL, COLS))
+        w2_quantise(j + 1)
+        mm2(j + 1)
         quarters = [slice(256 * a, 256 * (a + 1)) for a in range(4)]
         for a in range(4):
-            w2_interleave(d, TAIL_ENG[a], quarters[a])
-        h_quantise(d)
-        wq, ws = w2_quantise(d, first)
-        mm2_part(d, 0, 0, wq[:], ws[:])
-        halves = [w2_quantise(d, cols) for cols in quarters[2:]]
+            w2_interleave(j + 3, TAIL_ENG[a], quarters[a])
+        w2_quantise(j + 2)
+        mm2(j + 2)
+        wq, ws = w2_quantise_part(j + 3, first)
+        mm2_part(j + 3, 0, 0, wq[:], ws[:])
+        halves = [w2_quantise_part(j + 3, cols) for cols in quarters[2:]]
         store(E - 2)
         for a in range(2):
-            mm2_part(d, 1, a, halves[a][0][:], halves[a][1][:])
+            mm2_part(j + 3, 1, a, halves[a][0][:], halves[a][1][:])
         store(E - 1)

@@ -26,9 +26,8 @@ AHEAD = 3
 POOL_FIRST = 704
 POOL_COLS = 896
 V_COLS_HEAD = 896
-V_COLS = 512
-V_COLS_TAIL = 512
-TAIL_ENG = "vvss"
+V_COLS = 576
+V_COLS_TAIL = 384
 PARK = (E - 1) * TOK
 CLAMP_MAX = float(math.log(100.0))
 FLOPS = 2 * N * D * H * 2
@@ -228,11 +227,10 @@ def tile_moelayer_kernel(tc, x, W1, b1, W2_bytes, W2_scale, b2, temperature, out
             if k not in h_grp:
                 h_grp[k] = work.tile([P, G, 2, TOK, 4], BF16, name="h_grp", align_bytes=64, bufs=1)
             for i in range(2):
-                bias = b1_col[2 * k + i][:, g, 0:4].unsqueeze(1).unsqueeze(3)
+                bias = b1_col[2 * k + i][:, g, 0:4].unsqueeze(1)
                 nc.vector.tensor_tensor(
-                    out=h_grp[k][:, g, i].rearrange("p (c r) s -> p c s r", r=RUN),
-                    in0=h_ps[d, i][:].rearrange("p s (c r) -> p c s r", r=RUN),
-                    in1=bias.to_broadcast([P, TOK // RUN, 4, RUN]), op=ALU.add,
+                    out=h_grp[k][:, g, i], in0=h_ps[d, i][:].rearrange("p s t -> p t s"),
+                    in1=bias.to_broadcast([P, TOK, 4]), op=ALU.add,
                 )
 
         def h_relu(k):
@@ -242,10 +240,10 @@ def tile_moelayer_kernel(tc, x, W1, b1, W2_bytes, W2_scale, b2, temperature, out
         def h_quantise(k):
             h_cod[k] = quantise("h", h_grp[k][:].rearrange("p g i t s -> p (g i t s)"), G * 2 * TOK, 2)
 
-        def w2_widen(j, engine, cols=slice(0, COLS)):
+        def w2_widen(j, engine, cols=slice(0, COLS), slots=range(4)):
             if j not in w2_pl:
                 w2_pl[j] = work.tile([P, 4, COLS], BF16, name="w2_pl", align_bytes=64, bufs=3)
-            for s in range(4):
+            for s in slots:
                 src = w2_raw[j][:, s].rearrange("p i n -> p (i n)")[:, cols].bitcast(FP8)
                 dst = w2_pl[j][:, s, cols]
                 if engine == "v":
@@ -254,12 +252,12 @@ def tile_moelayer_kernel(tc, x, W1, b1, W2_bytes, W2_scale, b2, temperature, out
                     )
                 else:
                     nc.scalar.activation(out=dst, in_=src, func=ACT.Copy, scale=w2_scale(j % G, s))
-            if cols.stop == COLS:
+            if cols.stop == COLS and slots.stop == 4:
                 load_w2(j + AHEAD)
 
         def w2_tile(j):
             if j not in w2_grp:
-                w2_grp[j] = work.tile([P, COLS, 4], BF16, name="w2_grp", align_bytes=64, bufs=3)
+                w2_grp[j] = work.tile([P, COLS, 4], BF16, name="w2_grp", align_bytes=64, bufs=4)
             return w2_grp[j]
 
         def w2_interleave(j, engine, cols=slice(0, COLS)):
@@ -283,13 +281,13 @@ def tile_moelayer_kernel(tc, x, W1, b1, W2_bytes, W2_scale, b2, temperature, out
         def w2_quantise(j):
             w2_cod[j] = w2_quantise_part(j, slice(0, COLS))
 
-        def mm2_part(j, i, a, wq, ws):
+        def mm2_part(j, i, a, wq, ws, stop):
             k, g = divmod(j, G)
             hq, hs = h_cod[k]
             tok = slice((2 * g + i) * TOK, (2 * g + i + 1) * TOK)
             nc.tensor.matmul_mx(
                 out=y_ps[2 * k + i][a][:], lhsT=hq[:, tok].bitcast(FP8X4), lhsT_scale=hs[:, tok],
-                rhs=wq.bitcast(FP8X4), rhs_scale=ws, start=(g == 0), stop=(g == G - 1),
+                rhs=wq.bitcast(FP8X4), rhs_scale=ws, start=(g == 0), stop=stop,
             )
 
         def mm2(j):
@@ -304,36 +302,42 @@ def tile_moelayer_kernel(tc, x, W1, b1, W2_bytes, W2_scale, b2, temperature, out
                 width = D // len(y_ps[e])
                 for a in range(len(y_ps[e])):
                     cols = slice(i * D + a * width, i * D + (a + 1) * width)
-                    mm2_part(j, i, a, wq[:, cols], ws[:, cols])
+                    mm2_part(j, i, a, wq[:, cols], ws[:, cols], g == G - 1)
 
-        def store(e):
+        def store(e, a=0):
             width = D // len(y_ps[e])
-            for a, py in enumerate(y_ps[e]):
-                cols = slice(a * width, (a + 1) * width)
-                y = out_pool.tile([TOK, width], F32, name="y", align_bytes=64, bufs=3)
-                nc.vector.scalar_tensor_tensor(
-                    out=y[:], in0=py[:], scalar=gain[:], in1=b2_gain[e][:, cols],
-                    op0=ALU.mult, op1=ALU.add,
-                )
-                nc.sync.dma_start(out=out[e * TOK:(e + 1) * TOK, cols], in_=y[:])
+            cols = slice(a * width, (a + 1) * width)
+            y = out_pool.tile([TOK, width], F32, name="y", align_bytes=64, bufs=3)
+            nc.vector.scalar_tensor_tensor(
+                out=y[:], in0=y_ps[e][a][:], scalar=gain[:], in1=b2_gain[e][:, cols],
+                op0=ALU.mult, op1=ALU.add,
+            )
+            nc.sync.dma_start(out=out[e * TOK:(e + 1) * TOK, cols], in_=y[:])
 
         def window(k):
             d, j = G * k, 3 * k + 3
             pool_cols = POOL_FIRST if k == 0 else POOL_COLS
-            w2_widen(j, "v")
+            w2_widen(j, "v", slots=range(3, 4))
             w2_interleave_pool(j, slice(0, pool_cols))
             w2_interleave(j, "s", slice(pool_cols, COLS))
+            if k + 1 < PAIRS:
+                x_copy(k + 1)
             h_bias(d)
             mm1(d + 2)
             h_bias(d + 1)
             mm1(d + 3)
-            h_bias(d + 2)
-            h_bias(d + 3)
             if k > 0:
                 store(2 * k - 2)
                 store(2 * k - 1)
+            h_bias(d + 2)
+            h_bias(d + 3)
             load_b2(k)
+
+        def h_finish(k, j):
+            w2_widen(j, "v", slots=range(1))
             h_relu(k)
+            w2_widen(j, "v", slots=range(1, 4))
+            h_quantise(k)
 
         first, second = slice(0, D), slice(D, COLS)
         w2_widen(0, "v", first)
@@ -367,8 +371,10 @@ def tile_moelayer_kernel(tc, x, W1, b1, W2_bytes, W2_scale, b2, temperature, out
         w1_interleave(3)
         load_x(1)
         load_b1(1)
+        w2_widen(3, "v", slots=range(3))
         w2_quantise(2)
         w1_quantise(3)
+        x_turn(1)
         w1_interleave(4)
         window(0)
 
@@ -376,36 +382,35 @@ def tile_moelayer_kernel(tc, x, W1, b1, W2_bytes, W2_scale, b2, temperature, out
             d, j = G * k, 3 * k
             w1_interleave(d + 1)
             w1_to_psum(d + 2)
-            w2_widen(j + 1, "v")
-            h_quantise(k - 1)
+            h_finish(k - 1, j + 1)
+            w1_interleave(d + 2)
+            w1_to_psum(d + 3)
+            if k + 1 < PAIRS:
+                load_x(k + 1)
+                load_b1(k + 1)
             for ready in range(d - G, j):
                 mm2(ready)
-            w1_interleave(d + 2)
-            x_turn(k)
+            w2_widen(j + 2, "v")
             w2_quantise(j)
             if j < d:
                 mm2(j)
             w1_quantise(d)
-            w2_interleave(j + 1, "s")
-            x_copy(k)
-            w1_to_psum(d + 3)
-            w2_widen(j + 2, "v")
-            w1_quantise(d + 1)
             x_quantise(k)
-            w1_quantise(d + 2)
+            w1_quantise(d + 1)
             mm1(d)
             mm1(d + 1)
+            w2_interleave(j + 1, "s")
             w1_interleave(d + 3)
-            w1_to_psum(d + 4)
+            w2_interleave(j + 2, "v", slice(0, V_COLS))
+            w2_interleave(j + 2, "s", slice(V_COLS, COLS))
+            w1_quantise(d + 2)
             w2_quantise(j + 1)
             if j + 1 < d:
                 mm2(j + 1)
-            w2_interleave(j + 2, "v", slice(0, V_COLS))
-            w2_interleave(j + 2, "s", slice(V_COLS, COLS))
-            w1_quantise(d + 3)
             if k + 1 < PAIRS:
-                load_x(k + 1)
-                load_b1(k + 1)
+                x_turn(k + 1)
+            w2_widen(j + 3, "v", slots=range(3))
+            w1_quantise(d + 3)
             w2_quantise(j + 2)
             if j + 2 < d:
                 mm2(j + 2)
@@ -415,25 +420,29 @@ def tile_moelayer_kernel(tc, x, W1, b1, W2_bytes, W2_scale, b2, temperature, out
             window(k)
 
         j = STEPS - 4
+        halves = [slice(D + 256 * a, D + 256 * (a + 1)) for a in range(2)]
         w2_widen(j + 2, "s")
-        w2_widen(j + 3, "v")
-        h_quantise(PAIRS - 1)
+        h_finish(PAIRS - 1, j + 3)
         w2_quantise(j)
         mm2(j)
         w2_interleave(j + 1, "s")
-        w2_interleave(j + 2, "v", slice(0, V_COLS_TAIL))
-        w2_interleave(j + 2, "s", slice(V_COLS_TAIL, COLS))
+        w2_interleave(j + 3, "v", first)
         w2_quantise(j + 1)
         mm2(j + 1)
-        quarters = [slice(256 * a, 256 * (a + 1)) for a in range(4)]
-        for a in range(4):
-            w2_interleave(j + 3, TAIL_ENG[a], quarters[a])
-        w2_quantise(j + 2)
-        mm2(j + 2)
-        wq, ws = w2_quantise_part(j + 3, first)
-        mm2_part(j + 3, 0, 0, wq[:], ws[:])
-        halves = [w2_quantise_part(j + 3, cols) for cols in quarters[2:]]
-        store(E - 2)
+        w2_interleave(j + 2, "v", slice(0, V_COLS_TAIL))
+        w2_interleave(j + 2, "s", slice(V_COLS_TAIL, COLS))
+        for cols in halves:
+            w2_interleave(j + 3, "s", cols)
+        for step in (j + 3, j + 2):
+            wq, ws = w2_quantise_part(step, first)
+            mm2_part(step, 0, 0, wq[:], ws[:], step == j + 2)
+        wq, ws = w2_quantise_part(j + 2, second)
         for a in range(2):
-            mm2_part(j + 3, 1, a, halves[a][0][:], halves[a][1][:])
-        store(E - 1)
+            mm2_part(j + 2, 1, a, wq[:, 256 * a:256 * (a + 1)], ws[:, 256 * a:256 * (a + 1)], False)
+        for a in range(2):
+            wq, ws = w2_quantise_part(j + 3, halves[a])
+            mm2_part(j + 3, 1, a, wq[:], ws[:], True)
+            if a == 0:
+                store(E - 2)
+        store(E - 1, 0)
+        store(E - 1, 1)

@@ -22,11 +22,12 @@ STEPS = PAIRS * G
 COLS = 2 * D
 PE_STEPS = (6, 7, 10, 11, 14, 15)
 RUN = 2
+H_RUN = 4
 AHEAD = 3
-POOL_FIRST = 704
-POOL_COLS = 896
+POOL_FIRST = 832
+POOL_COLS = 1024
 V_COLS_HEAD = 896
-V_COLS = 576
+V_COLS = 448
 V_COLS_TAIL = 384
 PARK = (E - 1) * TOK
 CLAMP_MAX = float(math.log(100.0))
@@ -227,10 +228,11 @@ def tile_moelayer_kernel(tc, x, W1, b1, W2_bytes, W2_scale, b2, temperature, out
             if k not in h_grp:
                 h_grp[k] = work.tile([P, G, 2, TOK, 4], BF16, name="h_grp", align_bytes=64, bufs=1)
             for i in range(2):
-                bias = b1_col[2 * k + i][:, g, 0:4].unsqueeze(1)
+                bias = b1_col[2 * k + i][:, g, 0:4].unsqueeze(1).unsqueeze(3)
                 nc.vector.tensor_tensor(
-                    out=h_grp[k][:, g, i], in0=h_ps[d, i][:].rearrange("p s t -> p t s"),
-                    in1=bias.to_broadcast([P, TOK, 4]), op=ALU.add,
+                    out=h_grp[k][:, g, i].rearrange("p (c r) s -> p c s r", r=H_RUN),
+                    in0=h_ps[d, i][:].rearrange("p s (c r) -> p c s r", r=H_RUN),
+                    in1=bias.to_broadcast([P, TOK // H_RUN, 4, H_RUN]), op=ALU.add,
                 )
 
         def h_relu(k):

@@ -22,12 +22,11 @@ STEPS = PAIRS * G
 COLS = 2 * D
 PE_STEPS = (6, 7, 10, 11, 14, 15)
 RUN = 2
-H_RUN = 4
 AHEAD = 3
 POOL_FIRST = 832
 POOL_COLS = 1024
 V_COLS_HEAD = 896
-V_COLS = 448
+V_COLS = 384
 V_COLS_TAIL = 384
 PARK = (E - 1) * TOK
 CLAMP_MAX = float(math.log(100.0))
@@ -230,9 +229,9 @@ def tile_moelayer_kernel(tc, x, W1, b1, W2_bytes, W2_scale, b2, temperature, out
             for i in range(2):
                 bias = b1_col[2 * k + i][:, g, 0:4].unsqueeze(1).unsqueeze(3)
                 nc.vector.tensor_tensor(
-                    out=h_grp[k][:, g, i].rearrange("p (c r) s -> p c s r", r=H_RUN),
-                    in0=h_ps[d, i][:].rearrange("p s (c r) -> p c s r", r=H_RUN),
-                    in1=bias.to_broadcast([P, TOK // H_RUN, 4, H_RUN]), op=ALU.add,
+                    out=h_grp[k][:, g, i].rearrange("p (c r) s -> p c s r", r=RUN),
+                    in0=h_ps[d, i][:].rearrange("p s (c r) -> p c s r", r=RUN),
+                    in1=bias.to_broadcast([P, TOK // RUN, 4, RUN]), op=ALU.add,
                 )
 
         def h_relu(k):

@@ -23,10 +23,10 @@ COLS = 2 * D
 PE_STEPS = (6, 7, 10, 11, 14, 15)
 RUN = 2
 AHEAD = 3
-POOL_FIRST = 832
-POOL_COLS = 1024
+POOL_FIRST = 704
+POOL_COLS = 896
 V_COLS_HEAD = 896
-V_COLS = 384
+V_COLS = 448
 V_COLS_TAIL = 384
 PARK = (E - 1) * TOK
 CLAMP_MAX = float(math.log(100.0))

@@ -23,10 +23,11 @@ COLS = 2 * D
 PE_STEPS = (6, 7, 10, 11, 14, 15)
 RUN = 2
 AHEAD = 3
+LONG_ROWS = 2
 POOL_FIRST = 704
 POOL_COLS = 896
 V_COLS_HEAD = 896
-V_COLS = 448
+V_COLS = 640
 V_COLS_TAIL = 384
 PARK = (E - 1) * TOK
 CLAMP_MAX = float(math.log(100.0))
@@ -75,17 +76,18 @@ def tile_moelayer_kernel(tc, x, W1, b1, W2_bytes, W2_scale, b2, temperature, out
         def load_w2_part(j, i):
             k, g = divmod(j, G)
             if j not in w2_raw:
-                w2_raw[j] = raw_pool.tile([P, 4, 2, D], U8, name="w2_bytes", align_bytes=64)
+                shape = [P, 2, 4, D] if j < LONG_ROWS else [P, 4, 2, D]
+                w2_raw[j] = raw_pool.tile(shape, U8, name="w2_bytes", align_bytes=64)
             src = W2_bytes[2 * k + i].rearrange("(g p s) n -> p g s n", p=P, s=4)[:, g]
-            nc.sync.dma_start(out=w2_raw[j][:, :, i, :], in_=src)
+            nc.sync.dma_start(out=w2_raw[j][:, i] if j < LONG_ROWS else w2_raw[j][:, :, i, :], in_=src)
 
         def load_w1(d):
-            if d < STEPS:
+            if d < STEPS and d not in w1_raw:
                 load_w1_part(d, 0)
                 load_w1_part(d, 1)
 
         def load_w2(j):
-            if j < STEPS:
+            if j < STEPS and j not in w2_raw:
                 load_w2_part(j, 0)
                 load_w2_part(j, 1)
 
@@ -124,14 +126,18 @@ def tile_moelayer_kernel(tc, x, W1, b1, W2_bytes, W2_scale, b2, temperature, out
         load_w1_part(0, 1)
         load_w2_part(1, 0)
         nc.sync.dma_start(out=scale_rest[:, :, 0:4], in_=scale_src[:, 1:G, :])
-        load_w2_part(1, 1)
         load_w1_part(1, 0)
-        load_x(0)
+        load_w2_part(1, 1)
         load_w1_part(1, 1)
+        load_w1_part(2, 0)
         load_w2(2)
-        load_w1(2)
+        load_w1_part(2, 1)
+        load_x(0)
         nc.sync.dma_start(out=b2_rows[:], in_=b2)
+        load_w1(3)
         load_b1(0)
+        load_x(1)
+        load_w2(3)
 
         ident = const.tile([P, P], F32, name="ident", align_bytes=64)
         make_identity(nc, ident[:])
@@ -245,7 +251,10 @@ def tile_moelayer_kernel(tc, x, W1, b1, W2_bytes, W2_scale, b2, temperature, out
             if j not in w2_pl:
                 w2_pl[j] = work.tile([P, 4, COLS], BF16, name="w2_pl", align_bytes=64, bufs=3)
             for s in slots:
-                src = w2_raw[j][:, s].rearrange("p i n -> p (i n)")[:, cols].bitcast(FP8)
+                if j < LONG_ROWS:
+                    src = w2_raw[j][:, cols.start // D, s, :].bitcast(FP8)
+                else:
+                    src = w2_raw[j][:, s].rearrange("p i n -> p (i n)").bitcast(FP8)
                 dst = w2_pl[j][:, s, cols]
                 if engine == "v":
                     nc.vector.tensor_scalar(
@@ -346,31 +355,32 @@ def tile_moelayer_kernel(tc, x, W1, b1, W2_bytes, W2_scale, b2, temperature, out
         w1_copy(0, slice(0, 1), slice(0, 64))
         w1_copy(0, slice(0, 1), slice(64, P))
         w1_copy(0, slice(1, 2))
-        load_w1(AHEAD)
+        load_w1(4)
         w2_interleave(0, "v", first)
         w2_interleave(0, "v", second)
-        w2_widen(1, "v")
+        w2_widen(1, "v", first)
+        w2_widen(1, "v", second)
         w2_quantise(0)
         w1_quantise(0)
-        x_turn(0)
         w1_copy(1, slice(0, 1))
         w1_copy(1, slice(1, 2))
-        load_w1(1 + AHEAD)
-        x_copy(0)
         w2_interleave(1, "v")
         w2_widen(2, "v")
         w2_quantise(1)
         w1_quantise(1)
+        w1_copy(2, slice(0, 1))
+        w1_copy(2, slice(1, 2))
+        load_w1(2 + AHEAD)
+        x_turn(0)
+        x_copy(0)
+        w2_interleave(2, "v", slice(0, V_COLS_HEAD))
+        w2_interleave(2, "s", slice(V_COLS_HEAD, COLS))
         park_b2()
         x_quantise(0)
         mm1(0)
         mm1(1)
-        w1_interleave(2)
-        w2_interleave(2, "v", slice(0, V_COLS_HEAD))
-        w2_interleave(2, "s", slice(V_COLS_HEAD, COLS))
         w1_quantise(2)
         w1_interleave(3)
-        load_x(1)
         load_b1(1)
         w2_widen(3, "v", slots=range(3))
         w2_quantise(2)

@@ -24,11 +24,11 @@ PE_STEPS = (6, 7, 10, 11, 14, 15)
 RUN = 2
 AHEAD = 3
 LONG_ROWS = 2
-POOL_FIRST = 704
-POOL_COLS = 896
+POOL_FIRST = 832
+POOL_COLS = 1024
 V_COLS_HEAD = 896
-V_COLS = 640
-V_COLS_TAIL = 384
+V_COLS = 448
+V_COLS_TAIL = 320
 PARK = (E - 1) * TOK
 CLAMP_MAX = float(math.log(100.0))
 FLOPS = 2 * N * D * H * 2
@@ -174,7 +174,7 @@ def tile_moelayer_kernel(tc, x, W1, b1, W2_bytes, W2_scale, b2, temperature, out
 
         def w1_tile(d):
             if d not in w1_grp:
-                w1_grp[d] = work.tile([P, 2, 4, P, 4], BF16, name="w1_grp", align_bytes=64, bufs=3)
+                w1_grp[d] = work.tile([P, 2, 4, P, 4], BF16, name="w1_grp", align_bytes=64, bufs=4)
             return w1_grp[d]
 
         def w1_copy(d, experts, m=slice(0, P)):
@@ -328,6 +328,7 @@ def tile_moelayer_kernel(tc, x, W1, b1, W2_bytes, W2_scale, b2, temperature, out
             d, j = G * k, 3 * k + 3
             pool_cols = POOL_FIRST if k == 0 else POOL_COLS
             w2_widen(j, "v", slots=range(3, 4))
+            w1_quantise(d + 2)
             w2_interleave_pool(j, slice(0, pool_cols))
             w2_interleave(j, "s", slice(pool_cols, COLS))
             if k + 1 < PAIRS:
@@ -374,16 +375,14 @@ def tile_moelayer_kernel(tc, x, W1, b1, W2_bytes, W2_scale, b2, temperature, out
         x_turn(0)
         x_copy(0)
         w2_interleave(2, "v", slice(0, V_COLS_HEAD))
-        w2_interleave(2, "s", slice(V_COLS_HEAD, COLS))
         park_b2()
         x_quantise(0)
         mm1(0)
         mm1(1)
-        w1_quantise(2)
         w1_interleave(3)
+        w2_interleave(2, "s", slice(V_COLS_HEAD, COLS))
         load_b1(1)
         w2_widen(3, "v", slots=range(3))
-        w2_quantise(2)
         w1_quantise(3)
         x_turn(1)
         w1_interleave(4)
@@ -394,6 +393,7 @@ def tile_moelayer_kernel(tc, x, W1, b1, W2_bytes, W2_scale, b2, temperature, out
             w1_interleave(d + 1)
             w1_to_psum(d + 2)
             h_finish(k - 1, j + 1)
+            w2_quantise(j - 1)
             w1_interleave(d + 2)
             w1_to_psum(d + 3)
             if k + 1 < PAIRS:
@@ -414,7 +414,6 @@ def tile_moelayer_kernel(tc, x, W1, b1, W2_bytes, W2_scale, b2, temperature, out
             w1_interleave(d + 3)
             w2_interleave(j + 2, "v", slice(0, V_COLS))
             w2_interleave(j + 2, "s", slice(V_COLS, COLS))
-            w1_quantise(d + 2)
             w2_quantise(j + 1)
             if j + 1 < d:
                 mm2(j + 1)
@@ -422,11 +421,10 @@ def tile_moelayer_kernel(tc, x, W1, b1, W2_bytes, W2_scale, b2, temperature, out
                 x_turn(k + 1)
             w2_widen(j + 3, "v", slots=range(3))
             w1_quantise(d + 3)
-            w2_quantise(j + 2)
-            if j + 2 < d:
-                mm2(j + 2)
             w1_interleave(d + 4)
             if k == PAIRS - 1:
+                w2_quantise(j + 2)
+                mm2(j + 2)
                 w2_widen(STEPS - 3, "s")
             window(k)
 

@@ -178,10 +178,12 @@ def tile_moelayer_kernel(tc, x, W1, b1, W2_bytes, W2_scale, b2, temperature, out
             return w1_grp[d]
 
         def w1_copy(d, experts, m=slice(0, P)):
-            nc.scalar.copy(
-                out=w1_tile(d)[:, experts].rearrange("p i s m j -> p i m j s")[:, :, m],
-                in_=w1_raw[d][:, experts].rearrange("p i j (m s) -> p i m j s", s=4)[:, :, m],
-            )
+            pairs = slice(m.start // RUN, m.stop // RUN)
+            for i in range(experts.start, experts.stop):
+                nc.scalar.copy(
+                    out=w1_tile(d)[:, i].rearrange("p s (c r) j -> p c s j r", r=RUN)[:, pairs],
+                    in_=w1_raw[d][:, i].rearrange("p j (c r s) -> p c s j r", r=RUN, s=4)[:, pairs],
+                )
 
         def w1_to_psum(d):
             if d not in PE_STEPS:

@@ -26,9 +26,9 @@ AHEAD = 3
 LONG_ROWS = 2
 POOL_FIRST = 832
 POOL_COLS = 1024
-V_COLS_HEAD = 896
-V_COLS = 448
-V_COLS_TAIL = 320
+V_COLS_HEAD = 768
+V_COLS = 320
+V_COLS_TAIL = 192
 PARK = (E - 1) * TOK
 CLAMP_MAX = float(math.log(100.0))
 FLOPS = 2 * N * D * H * 2

@@ -26,9 +26,10 @@ AHEAD = 3
 LONG_ROWS = 2
 POOL_FIRST = 832
 POOL_COLS = 1024
-V_COLS_HEAD = 768
+V_COLS_HEAD = 704
 V_COLS = 320
-V_COLS_TAIL = 192
+V_COLS_TAIL = 128
+PE_COLS = 192
 PARK = (E - 1) * TOK
 CLAMP_MAX = float(math.log(100.0))
 FLOPS = 2 * N * D * H * 2
@@ -280,6 +281,20 @@ def tile_moelayer_kernel(tc, x, W1, b1, W2_bytes, W2_scale, b2, temperature, out
                     w2_pl[j][:, :, cols].rearrange("p s (c r) -> p c s r", r=RUN),
                 )
 
+        def w2_through_psum(j, cols):
+            src = w2_pl[j][:].rearrange("p s c -> p c s")
+            bank = ps_t.tile([P, cols.stop - cols.start, 4], BF16, name="tp")
+            for lo in range(cols.start, cols.stop, P):
+                hi = min(lo + P, cols.stop)
+                nc.tensor.matmul(
+                    out=bank[:, lo - cols.start:hi - cols.start, :].rearrange("p c s -> p (c s)"),
+                    lhsT=ident_bf[:], rhs=src[:, lo:hi, :], start=True, stop=True,
+                )
+            nc.scalar.copy(
+                out=w2_tile(j)[:, cols, :].rearrange("p c s -> p (c s)").bitcast(F32),
+                in_=bank[:].rearrange("p c s -> p (c s)").bitcast(F32),
+            )
+
         def w2_interleave_pool(j, cols):
             nc.gpsimd.tensor_scalar(
                 out=w2_tile(j)[:, cols, :], in0=w2_pl[j][:, :, cols].rearrange("p s c -> p c s"),
@@ -316,12 +331,13 @@ def tile_moelayer_kernel(tc, x, W1, b1, W2_bytes, W2_scale, b2, temperature, out
                     cols = slice(i * D + a * width, i * D + (a + 1) * width)
                     mm2_part(j, i, a, wq[:, cols], ws[:, cols], g == G - 1)
 
-        def store(e, a=0):
-            width = D // len(y_ps[e])
+        def store(e, a=0, parts=1):
+            width = D // parts
             cols = slice(a * width, (a + 1) * width)
-            y = out_pool.tile([TOK, width], F32, name="y", align_bytes=64, bufs=3)
+            bank = y_ps[e][a][:] if len(y_ps[e]) > 1 else y_ps[e][0][:, cols]
+            y = out_pool.tile([TOK, width], F32, name="y", align_bytes=64, bufs=4)
             nc.vector.scalar_tensor_tensor(
-                out=y[:], in0=y_ps[e][a][:], scalar=gain[:], in1=b2_gain[e][:, cols],
+                out=y[:], in0=bank, scalar=gain[:], in1=b2_gain[e][:, cols],
                 op0=ALU.mult, op1=ALU.add,
             )
             nc.sync.dma_start(out=out[e * TOK:(e + 1) * TOK, cols], in_=y[:])
@@ -415,7 +431,10 @@ def tile_moelayer_kernel(tc, x, W1, b1, W2_bytes, W2_scale, b2, temperature, out
             w2_interleave(j + 1, "s")
             w1_interleave(d + 3)
             w2_interleave(j + 2, "v", slice(0, V_COLS))
-            w2_interleave(j + 2, "s", slice(V_COLS, COLS))
+            pe_cols = PE_COLS if k == PAIRS - 1 else 0
+            w2_interleave(j + 2, "s", slice(V_COLS, COLS - pe_cols))
+            if pe_cols:
+                w2_through_psum(j + 2, slice(COLS - pe_cols, COLS))
             w2_quantise(j + 1)
             if j + 1 < d:
                 mm2(j + 1)
@@ -453,7 +472,6 @@ def tile_moelayer_kernel(tc, x, W1, b1, W2_bytes, W2_scale, b2, temperature, out
         for a in range(2):
             wq, ws = w2_quantise_part(j + 3, halves[a])
             mm2_part(j + 3, 1, a, wq[:], ws[:], True)
-            if a == 0:
-                store(E - 2)
-        store(E - 1, 0)
-        store(E - 1, 1)
+            store(E - 2, a, 2)
+        for a in range(2):
+            store(E - 1, a, 2)

@@ -24,11 +24,12 @@ PE_STEPS = (6, 7, 10, 11, 14, 15)
 RUN = 2
 AHEAD = 3
 LONG_ROWS = 2
-POOL_FIRST = 832
+POOL_FIRST = 896
+POOL_EXTRA = 64
 POOL_COLS = 1024
-V_COLS_HEAD = 704
+V_COLS_HEAD = 640
 V_COLS = 320
-V_COLS_TAIL = 128
+V_COLS_TAIL = 64
 PE_COLS = 192
 PARK = (E - 1) * TOK
 CLAMP_MAX = float(math.log(100.0))
@@ -348,6 +349,8 @@ def tile_moelayer_kernel(tc, x, W1, b1, W2_bytes, W2_scale, b2, temperature, out
             w2_widen(j, "v", slots=range(3, 4))
             w1_quantise(d + 2)
             w2_interleave_pool(j, slice(0, pool_cols))
+            if k > 0:
+                w2_interleave_pool(j + 1 if k == PAIRS - 1 else j - 1, slice(0, POOL_EXTRA))
             w2_interleave(j, "s", slice(pool_cols, COLS))
             if k + 1 < PAIRS:
                 x_copy(k + 1)
@@ -430,7 +433,7 @@ def tile_moelayer_kernel(tc, x, W1, b1, W2_bytes, W2_scale, b2, temperature, out
             mm1(d + 1)
             w2_interleave(j + 1, "s")
             w1_interleave(d + 3)
-            w2_interleave(j + 2, "v", slice(0, V_COLS))
+            w2_interleave(j + 2, "v", slice(0 if k == PAIRS - 1 else POOL_EXTRA, V_COLS))
             pe_cols = PE_COLS if k == PAIRS - 1 else 0
             w2_interleave(j + 2, "s", slice(V_COLS, COLS - pe_cols))
             if pe_cols:
@@ -455,7 +458,7 @@ def tile_moelayer_kernel(tc, x, W1, b1, W2_bytes, W2_scale, b2, temperature, out
         h_finish(PAIRS - 1, j + 3)
         w2_quantise(j)
         mm2(j)
-        w2_interleave(j + 1, "s")
+        w2_interleave(j + 1, "s", slice(POOL_EXTRA, COLS))
         w2_interleave(j + 3, "v", first)
         w2_quantise(j + 1)
         mm2(j + 1)

@@ -298,7 +298,8 @@ def tile_moelayer_kernel(tc, x, W1, b1, W2_bytes, W2_scale, b2, temperature, out
 
         def w2_interleave_pool(j, cols):
             nc.gpsimd.tensor_scalar(
-                out=w2_tile(j)[:, cols, :], in0=w2_pl[j][:, :, cols].rearrange("p s c -> p c s"),
+                out=w2_tile(j)[:, cols, :].rearrange("p (c r) s -> p c s r", r=RUN),
+                in0=w2_pl[j][:, :, cols].rearrange("p s (c r) -> p c s r", r=RUN),
                 scalar1=1.0, scalar2=0.0, op0=ALU.mult, op1=ALU.add,
             )
 

@@ -20,13 +20,11 @@ G = H // 512
 PAIRS = E // 2
 STEPS = PAIRS * G
 COLS = 2 * D
-PE_STEPS = (6, 7, 10, 11, 14, 15)
 RUN = 2
 AHEAD = 3
 LONG_ROWS = 2
-POOL_FIRST = 896
-POOL_EXTRA = 64
-POOL_COLS = 1024
+POOL_FIRST = 944
+POOL_EXTRA = 112
 V_COLS_HEAD = 640
 V_COLS = 320
 V_COLS_TAIL = 64
@@ -56,12 +54,6 @@ def tile_moelayer_kernel(tc, x, W1, b1, W2_bytes, W2_scale, b2, temperature, out
         x_rows, x_ps, x_grp, x_cod = {}, {}, {}, {}
         b1_col, b2_gain, y_ps = {}, {}, {}
 
-        def copy(engine, dst, src):
-            if engine == "v":
-                nc.vector.tensor_copy(out=dst, in_=src)
-            else:
-                nc.scalar.copy(out=dst, in_=src)
-
         def quantise(name, grp, width, bufs):
             q = codes.tile([P, width], U32, name=name + "_q", align_bytes=64, bufs=bufs)
             sc = codes.tile([P, width], U8, name=name + "_s", align_bytes=64, bufs=bufs)
@@ -72,7 +64,7 @@ def tile_moelayer_kernel(tc, x, W1, b1, W2_bytes, W2_scale, b2, temperature, out
             k, g = divmod(d, G)
             if d not in w1_raw:
                 w1_raw[d] = raw_pool.tile([P, 2, 4, 512], BF16, name="w1_raw", align_bytes=64)
-            src = W1[2 * k + i].rearrange("(p j) (g c) -> p g j c", j=4, c=512)[:, g]
+            src = W1[2 * k + i].rearrange("(p t) (g c) -> p g t c", t=4, c=512)[:, g]
             nc.sync.dma_start(out=w1_raw[d][:, i, :, cols], in_=src[:, :, cols])
 
         def load_w2_part(j, i):
@@ -183,14 +175,15 @@ def tile_moelayer_kernel(tc, x, W1, b1, W2_bytes, W2_scale, b2, temperature, out
             pairs = slice(m.start // RUN, m.stop // RUN)
             for i in range(experts.start, experts.stop):
                 nc.scalar.copy(
-                    out=w1_tile(d)[:, i].rearrange("p s (c r) j -> p c s j r", r=RUN)[:, pairs],
-                    in_=w1_raw[d][:, i].rearrange("p j (c r s) -> p c s j r", r=RUN, s=4)[:, pairs],
+                    out=w1_tile(d)[:, i].rearrange("p s (c r) t -> p c s t r", r=RUN)[:, pairs],
+                    in_=w1_raw[d][:, i].rearrange("p t (c r s) -> p c s t r", r=RUN, s=4)[:, pairs],
                 )
 
+        def through_psum(d):
+            return d >= G and d % G >= 2
+
         def w1_to_psum(d):
-            if d not in PE_STEPS:
-                return
-            src = w1_raw[d][:, 1].rearrange("p j (m s) -> p s m j", s=4)
+            src = w1_raw[d][:, 1].rearrange("p t (m s) -> p s m t", s=4)
             w1_ps[d] = []
             for a in range(2):
                 bank = ps_t.tile([P, 2, 512], BF16, name="tp")
@@ -203,9 +196,9 @@ def tile_moelayer_kernel(tc, x, W1, b1, W2_bytes, W2_scale, b2, temperature, out
         def w1_interleave(d):
             if d >= STEPS:
                 return
-            if d in PE_STEPS:
+            if through_psum(d):
                 w1_copy(d, slice(0, 1))
-                dst = w1_tile(d)[:, 1].rearrange("p s m j -> p (s m j)")
+                dst = w1_tile(d)[:, 1].rearrange("p s m t -> p (s m t)")
                 for a, bank in enumerate(w1_ps[d]):
                     nc.scalar.copy(
                         out=dst[:, 1024 * a:1024 * (a + 1)].bitcast(F32),
@@ -216,7 +209,7 @@ def tile_moelayer_kernel(tc, x, W1, b1, W2_bytes, W2_scale, b2, temperature, out
             load_w1(d + AHEAD)
 
         def w1_quantise(d):
-            w1_cod[d] = quantise("w1", w1_grp[d][:].rearrange("p i s m j -> p (i s m j)"), 1024, G)
+            w1_cod[d] = quantise("w1", w1_grp[d][:].rearrange("p i s m t -> p (i s m t)"), 1024, G)
 
         def mm1(d):
             q, sc = w1_cod[d]
@@ -245,11 +238,11 @@ def tile_moelayer_kernel(tc, x, W1, b1, W2_bytes, W2_scale, b2, temperature, out
                 )
 
         def h_relu(k):
-            flat = h_grp[k][:].rearrange("p g i t s -> p (g i t s)")
+            flat = h_grp[k][:].rearrange("p g i r s -> p (g i r s)")
             nc.vector.tensor_scalar_max(flat, flat, 0.0)
 
         def h_quantise(k):
-            h_cod[k] = quantise("h", h_grp[k][:].rearrange("p g i t s -> p (g i t s)"), G * 2 * TOK, 2)
+            h_cod[k] = quantise("h", h_grp[k][:].rearrange("p g i r s -> p (g i r s)"), G * 2 * TOK, 2)
 
         def w2_widen(j, engine, cols=slice(0, COLS), slots=range(4)):
             if j not in w2_pl:
@@ -260,7 +253,7 @@ def tile_moelayer_kernel(tc, x, W1, b1, W2_bytes, W2_scale, b2, temperature, out
                 else:
                     src = w2_raw[j][:, s].rearrange("p i n -> p (i n)").bitcast(FP8)
                 dst = w2_pl[j][:, s, cols]
-                if engine == "v":
+                if engine == "vector":
                     nc.vector.tensor_scalar(
                         out=dst, in0=src, scalar1=w2_scale(j % G, s), scalar2=None, op0=ALU.mult
                     )
@@ -275,12 +268,14 @@ def tile_moelayer_kernel(tc, x, W1, b1, W2_bytes, W2_scale, b2, temperature, out
             return w2_grp[j]
 
         def w2_interleave(j, engine, cols=slice(0, COLS)):
-            if cols.start < cols.stop:
-                copy(
-                    engine,
-                    w2_tile(j)[:, cols, :].rearrange("p (c r) s -> p c s r", r=RUN),
-                    w2_pl[j][:, :, cols].rearrange("p s (c r) -> p c s r", r=RUN),
-                )
+            dst = w2_tile(j)[:, cols, :].rearrange("p (c r) s -> p c s r", r=RUN)
+            src = w2_pl[j][:, :, cols].rearrange("p s (c r) -> p c s r", r=RUN)
+            if engine == "vector":
+                nc.vector.tensor_copy(out=dst, in_=src)
+            elif engine == "scalar":
+                nc.scalar.copy(out=dst, in_=src)
+            else:
+                nc.gpsimd.tensor_scalar(out=dst, in0=src, scalar1=1.0, scalar2=0.0, op0=ALU.mult, op1=ALU.add)
 
         def w2_through_psum(j, cols):
             src = w2_pl[j][:].rearrange("p s c -> p c s")
@@ -296,16 +291,9 @@ def tile_moelayer_kernel(tc, x, W1, b1, W2_bytes, W2_scale, b2, temperature, out
                 in_=bank[:].rearrange("p c s -> p (c s)").bitcast(F32),
             )
 
-        def w2_interleave_pool(j, cols):
-            nc.gpsimd.tensor_scalar(
-                out=w2_tile(j)[:, cols, :].rearrange("p (c r) s -> p c s r", r=RUN),
-                in0=w2_pl[j][:, :, cols].rearrange("p s (c r) -> p c s r", r=RUN),
-                scalar1=1.0, scalar2=0.0, op0=ALU.mult, op1=ALU.add,
-            )
-
         def w2_quantise_part(j, cols):
             grp = w2_grp[j][:, cols, :].rearrange("p n s -> p (n s)")
-            return quantise("w2", grp, cols.stop - cols.start, 4)
+            return quantise("w2", grp, cols.stop - cols.start, G)
 
         def w2_quantise(j):
             w2_cod[j] = w2_quantise_part(j, slice(0, COLS))
@@ -327,7 +315,7 @@ def tile_moelayer_kernel(tc, x, W1, b1, W2_bytes, W2_scale, b2, temperature, out
                 if g == 0 and e < E - 1:
                     y_ps[e] = [ps_y.tile([TOK, D], F32, name="py")]
                 if g == 0 and e == E - 1:
-                    y_ps[e] = [ps_y.tile([TOK, 256], F32, name="py"), ps_h.tile([TOK, 256], F32, name="ph")]
+                    y_ps[e] = [ps_y.tile([TOK, D // 2], F32, name="py"), ps_h.tile([TOK, D // 2], F32, name="ph")]
                 width = D // len(y_ps[e])
                 for a in range(len(y_ps[e])):
                     cols = slice(i * D + a * width, i * D + (a + 1) * width)
@@ -346,13 +334,14 @@ def tile_moelayer_kernel(tc, x, W1, b1, W2_bytes, W2_scale, b2, temperature, out
 
         def window(k):
             d, j = G * k, 3 * k + 3
-            pool_cols = POOL_FIRST if k == 0 else POOL_COLS
-            w2_widen(j, "v", slots=range(3, 4))
+            w2_widen(j, "vector", slots=range(3, 4))
             w1_quantise(d + 2)
-            w2_interleave_pool(j, slice(0, pool_cols))
-            if k > 0:
-                w2_interleave_pool(j + 1 if k == PAIRS - 1 else j - 1, slice(0, POOL_EXTRA))
-            w2_interleave(j, "s", slice(pool_cols, COLS))
+            if k == 0:
+                w2_interleave(j, "gpsimd", slice(0, POOL_FIRST))
+                w2_interleave(j, "scalar", slice(POOL_FIRST, COLS))
+            else:
+                w2_interleave(j, "gpsimd")
+                w2_interleave(j + 1 if k == PAIRS - 1 else j - 1, "gpsimd", slice(0, POOL_EXTRA))
             if k + 1 < PAIRS:
                 x_copy(k + 1)
             h_bias(d)
@@ -367,28 +356,28 @@ def tile_moelayer_kernel(tc, x, W1, b1, W2_bytes, W2_scale, b2, temperature, out
             load_b2(k)
 
         def h_finish(k, j):
-            w2_widen(j, "v", slots=range(1))
+            w2_widen(j, "vector", slots=range(1))
             h_relu(k)
-            w2_widen(j, "v", slots=range(1, 4))
+            w2_widen(j, "vector", slots=range(1, 4))
             h_quantise(k)
 
         first, second = slice(0, D), slice(D, COLS)
-        w2_widen(0, "v", first)
-        w2_widen(0, "v", second)
+        w2_widen(0, "vector", first)
+        w2_widen(0, "vector", second)
         w1_copy(0, slice(0, 1), slice(0, 64))
         w1_copy(0, slice(0, 1), slice(64, P))
         w1_copy(0, slice(1, 2))
-        load_w1(4)
-        w2_interleave(0, "v", first)
-        w2_interleave(0, "v", second)
-        w2_widen(1, "v", first)
-        w2_widen(1, "v", second)
+        load_w1(AHEAD + 1)
+        w2_interleave(0, "vector", first)
+        w2_interleave(0, "vector", second)
+        w2_widen(1, "vector", first)
+        w2_widen(1, "vector", second)
         w2_quantise(0)
         w1_quantise(0)
         w1_copy(1, slice(0, 1))
         w1_copy(1, slice(1, 2))
-        w2_interleave(1, "v")
-        w2_widen(2, "v")
+        w2_interleave(1, "vector")
+        w2_widen(2, "vector")
         w2_quantise(1)
         w1_quantise(1)
         w1_copy(2, slice(0, 1))
@@ -396,15 +385,15 @@ def tile_moelayer_kernel(tc, x, W1, b1, W2_bytes, W2_scale, b2, temperature, out
         load_w1(2 + AHEAD)
         x_turn(0)
         x_copy(0)
-        w2_interleave(2, "v", slice(0, V_COLS_HEAD))
+        w2_interleave(2, "vector", slice(0, V_COLS_HEAD))
         park_b2()
         x_quantise(0)
         mm1(0)
         mm1(1)
         w1_interleave(3)
-        w2_interleave(2, "s", slice(V_COLS_HEAD, COLS))
+        w2_interleave(2, "scalar", slice(V_COLS_HEAD, COLS))
         load_b1(1)
-        w2_widen(3, "v", slots=range(3))
+        w2_widen(3, "vector", slots=range(3))
         w1_quantise(3)
         x_turn(1)
         w1_interleave(4)
@@ -412,70 +401,73 @@ def tile_moelayer_kernel(tc, x, W1, b1, W2_bytes, W2_scale, b2, temperature, out
 
         for k in range(1, PAIRS):
             d, j = G * k, 3 * k
+            last = k == PAIRS - 1
             w1_interleave(d + 1)
             w1_to_psum(d + 2)
             h_finish(k - 1, j + 1)
             w2_quantise(j - 1)
             w1_interleave(d + 2)
             w1_to_psum(d + 3)
-            if k + 1 < PAIRS:
+            if not last:
                 load_x(k + 1)
                 load_b1(k + 1)
             for ready in range(d - G, j):
                 mm2(ready)
-            w2_widen(j + 2, "v")
+            w2_widen(j + 2, "vector")
             w2_quantise(j)
-            if j < d:
-                mm2(j)
+            mm2(j)
             w1_quantise(d)
             x_quantise(k)
             w1_quantise(d + 1)
             mm1(d)
             mm1(d + 1)
-            w2_interleave(j + 1, "s")
+            w2_interleave(j + 1, "scalar")
             w1_interleave(d + 3)
-            w2_interleave(j + 2, "v", slice(0 if k == PAIRS - 1 else POOL_EXTRA, V_COLS))
-            pe_cols = PE_COLS if k == PAIRS - 1 else 0
-            w2_interleave(j + 2, "s", slice(V_COLS, COLS - pe_cols))
-            if pe_cols:
-                w2_through_psum(j + 2, slice(COLS - pe_cols, COLS))
+            if last:
+                w2_interleave(j + 2, "vector", slice(0, V_COLS))
+                w2_interleave(j + 2, "scalar", slice(V_COLS, COLS - PE_COLS))
+                w2_through_psum(j + 2, slice(COLS - PE_COLS, COLS))
+            else:
+                w2_interleave(j + 2, "vector", slice(POOL_EXTRA, V_COLS))
+                w2_interleave(j + 2, "scalar", slice(V_COLS, COLS))
             w2_quantise(j + 1)
             if j + 1 < d:
                 mm2(j + 1)
-            if k + 1 < PAIRS:
+            if not last:
                 x_turn(k + 1)
-            w2_widen(j + 3, "v", slots=range(3))
+            w2_widen(j + 3, "vector", slots=range(3))
             w1_quantise(d + 3)
             w1_interleave(d + 4)
-            if k == PAIRS - 1:
+            if last:
                 w2_quantise(j + 2)
                 mm2(j + 2)
-                w2_widen(STEPS - 3, "s")
+                w2_widen(j + 4, "scalar")
             window(k)
 
-        j = STEPS - 4
-        halves = [slice(D + 256 * a, D + 256 * (a + 1)) for a in range(2)]
-        w2_widen(j + 2, "s")
+        j = STEPS - G
+        half = D // 2
+        halves = [slice(D + half * a, D + half * (a + 1)) for a in range(2)]
+        w2_widen(j + 2, "scalar")
         h_finish(PAIRS - 1, j + 3)
         w2_quantise(j)
         mm2(j)
-        w2_interleave(j + 1, "s", slice(POOL_EXTRA, COLS))
-        w2_interleave(j + 3, "v", first)
+        w2_interleave(j + 1, "scalar", slice(POOL_EXTRA, COLS))
         w2_quantise(j + 1)
         mm2(j + 1)
-        w2_interleave(j + 2, "v", slice(0, V_COLS_TAIL))
-        w2_interleave(j + 2, "s", slice(V_COLS_TAIL, COLS))
+        w2_interleave(j + 2, "vector", slice(0, V_COLS_TAIL))
+        w2_interleave(j + 3, "vector", first)
+        w2_interleave(j + 2, "scalar", slice(V_COLS_TAIL, COLS))
         for cols in halves:
-            w2_interleave(j + 3, "s", cols)
-        for step in (j + 3, j + 2):
+            w2_interleave(j + 3, "scalar", cols)
+        for step in (j + 2, j + 3):
             wq, ws = w2_quantise_part(step, first)
-            mm2_part(step, 0, 0, wq[:], ws[:], step == j + 2)
+            mm2_part(step, 0, 0, wq[:], ws[:], step == j + 3)
         wq, ws = w2_quantise_part(j + 2, second)
         for a in range(2):
-            mm2_part(j + 2, 1, a, wq[:, 256 * a:256 * (a + 1)], ws[:, 256 * a:256 * (a + 1)], False)
+            mm2_part(j + 2, 1, a, wq[:, half * a:half * (a + 1)], ws[:, half * a:half * (a + 1)], False)
         for a in range(2):
             wq, ws = w2_quantise_part(j + 3, halves[a])
             mm2_part(j + 3, 1, a, wq[:], ws[:], True)
-            store(E - 2, a, 2)
-        for a in range(2):
-            store(E - 1, a, 2)
+        for e in (E - 2, E - 1):
+            for a in range(2):
+                store(e, a, 2)

import math
from contextlib import ExitStack

import concourse.mybir as mybir
from concourse.masks import make_identity

F32 = mybir.dt.float32
BF16 = mybir.dt.bfloat16
U32 = mybir.dt.uint32
U8 = mybir.dt.uint8
FP8 = mybir.dt.float8_e4m3fn
FP8X4 = mybir.dt.float8_e4m3fn_x4
ALU = mybir.AluOpType
ACT = mybir.ActivationFunctionType

N, D, H, E = 1024, 512, 2048, 8
P = 128
TOK = N // E
G = H // 512
PAIRS = E // 2
STEPS = PAIRS * G
COLS = 2 * D
RUN = 2
AHEAD = 3
LONG_ROWS = 2
POOL_FIRST = 944
POOL_EXTRA = 112
V_COLS_HEAD = 640
V_COLS = 320
V_COLS_TAIL = 64
PE_COLS = 192
PARK = (E - 1) * TOK
CLAMP_MAX = float(math.log(100.0))
FLOPS = 2 * N * D * H * 2


def tile_moelayer_kernel(tc, x, W1, b1, W2_bytes, W2_scale, b2, temperature, out):
    nc = tc.nc

    with ExitStack() as ctx:
        ctx.enter_context(tc.manual_schedule())
        const = ctx.enter_context(tc.tile_pool(name="const", bufs=1))
        raw_pool = ctx.enter_context(tc.tile_pool(name="raw_pool", bufs=AHEAD + 1))
        work = ctx.enter_context(tc.tile_pool(name="work", bufs=2))
        codes = ctx.enter_context(tc.tile_pool(name="codes", bufs=2))
        out_pool = ctx.enter_context(tc.tile_pool(name="out_pool", bufs=2))
        ps_t = ctx.enter_context(tc.psum_pool(name="ps_t", bufs=2))
        ps_h = ctx.enter_context(tc.psum_pool(name="ps_h", bufs=4))
        ps_y = ctx.enter_context(tc.psum_pool(name="ps_y", bufs=2))

        w1_raw, w1_ps, w1_grp, w1_cod = {}, {}, {}, {}
        w2_raw, w2_pl, w2_grp, w2_cod = {}, {}, {}, {}
        h_ps, h_grp, h_cod = {}, {}, {}
        x_rows, x_ps, x_grp, x_cod = {}, {}, {}, {}
        b1_col, b2_gain, y_ps = {}, {}, {}

        def quantise(name, grp, width, bufs):
            q = codes.tile([P, width], U32, name=name + "_q", align_bytes=64, bufs=bufs)
            sc = codes.tile([P, width], U8, name=name + "_s", align_bytes=64, bufs=bufs)
            nc.vector.quantize_mx(out=q[:].bitcast(FP8X4), scales=sc[:], in_=grp)
            return q, sc

        def load_w1_part(d, i, cols=slice(0, 512)):
            k, g = divmod(d, G)
            if d not in w1_raw:
                w1_raw[d] = raw_pool.tile([P, 2, 4, 512], BF16, name="w1_raw", align_bytes=64)
            src = W1[2 * k + i].rearrange("(p t) (g c) -> p g t c", t=4, c=512)[:, g]
            nc.sync.dma_start(out=w1_raw[d][:, i, :, cols], in_=src[:, :, cols])

        def load_w2_part(j, i):
            k, g = divmod(j, G)
            if j not in w2_raw:
                shape = [P, 2, 4, D] if j < LONG_ROWS else [P, 4, 2, D]
                w2_raw[j] = raw_pool.tile(shape, U8, name="w2_bytes", align_bytes=64)
            src = W2_bytes[2 * k + i].rearrange("(g p s) n -> p g s n", p=P, s=4)[:, g]
            nc.sync.dma_start(out=w2_raw[j][:, i] if j < LONG_ROWS else w2_raw[j][:, :, i, :], in_=src)

        def load_w1(d):
            if d < STEPS and d not in w1_raw:
                load_w1_part(d, 0)
                load_w1_part(d, 1)

        def load_w2(j):
            if j < STEPS and j not in w2_raw:
                load_w2_part(j, 0)
                load_w2_part(j, 1)

        def load_x(k):
            x_rows[k] = work.tile([P, 2, D], BF16, name="x_rows", align_bytes=64)
            src = x.rearrange("(e p) d -> p e d", p=P)
            nc.sync.dma_start(out=x_rows[k][:], in_=src[:, 2 * k:2 * k + 2, :])

        def load_b1(k):
            for e in (2 * k, 2 * k + 1):
                b1_col[e] = out_pool.tile([P, G, 16], BF16, name="b1_col", align_bytes=64, bufs=4)
                nc.sync.dma_start(
                    out=b1_col[e][:, :, 0:4], in_=b1[e].rearrange("(g p s) -> p g s", p=P, s=4)
                )

        def load_b2(k):
            for e in (2 * k, 2 * k + 1):
                b2_gain[e] = out_pool.tile([P, D], F32, name="b2_gain", align_bytes=64)
                nc.sync.dma_start(out=b2_gain[e][:], in_=out[PARK + e, :].partition_broadcast(P))

        temp = const.tile([P, 1], BF16, name="temp", align_bytes=64)
        scale_head = const.tile([P, 4], F32, name="scale_head", align_bytes=64)
        scale_rest = const.tile([P, G - 1, 8], F32, name="scale_rest", align_bytes=64)
        b2_rows = const.tile([E, D], BF16, name="b2_rows", align_bytes=64)
        scale_src = W2_scale.rearrange("o (g p s) z -> p g (o s z)", p=P, s=4)

        def w2_scale(g, s):
            return scale_head[:, s:s + 1] if g == 0 else scale_rest[:, g - 1, s:s + 1]

        nc.sync.dma_start(out=temp[:], in_=temperature.partition_broadcast(P))
        nc.sync.dma_start(out=scale_head[:], in_=scale_src[:, 0, :])
        load_w2_part(0, 0)
        load_w1_part(0, 0, slice(0, 256))
        load_w2_part(0, 1)
        load_w1_part(0, 0, slice(256, 512))
        load_w1_part(0, 1)
        load_w2_part(1, 0)
        nc.sync.dma_start(out=scale_rest[:, :, 0:4], in_=scale_src[:, 1:G, :])
        load_w1_part(1, 0)
        load_w2_part(1, 1)
        load_w1_part(1, 1)
        load_w1_part(2, 0)
        load_w2(2)
        load_w1_part(2, 1)
        load_x(0)
        nc.sync.dma_start(out=b2_rows[:], in_=b2)
        load_w1(3)
        load_b1(0)
        load_x(1)
        load_w2(3)

        ident = const.tile([P, P], F32, name="ident", align_bytes=64)
        make_identity(nc, ident[:])
        ident_bf = const.tile([P, P], BF16, name="ident_bf", align_bytes=64)
        make_identity(nc, ident_bf[:])

        clamped = const.tile([P, 1], F32, name="clamped", align_bytes=64)
        gain = const.tile([P, 1], F32, name="gain", align_bytes=64)
        nc.vector.tensor_scalar_min(clamped[:], temp[:], CLAMP_MAX)
        nc.scalar.activation(out=gain[:], in_=clamped[:], func=ACT.Exp)

        def park_b2():
            rows = const.tile([E, D], F32, name="b2_scaled", align_bytes=64)
            nc.vector.tensor_scalar(
                out=rows[:], in0=b2_rows[:], scalar1=gain[0:E, :], scalar2=None, op0=ALU.mult
            )
            nc.sync.dma_start(out=out[PARK:PARK + E, :], in_=rows[:])

        def x_turn(k):
            x_ps[k] = ps_t.tile([P, 4, P], F32, name="tp")
            for i in range(2):
                words = x_rows[k][:, i, :].bitcast(F32)
                for u in range(2):
                    nc.tensor.transpose(x_ps[k][:, 2 * i + u, :], words[:, u:256:2], ident[:])

        def x_copy(k):
            x_grp[k] = work.tile([P, 2, TOK, 4], BF16, name="x_grp", align_bytes=64, bufs=1)
            nc.scalar.copy(
                out=x_grp[k][:].bitcast(F32), in_=x_ps[k][:].rearrange("p (i u) r -> p i r u", u=2)
            )

        def x_quantise(k):
            x_cod[k] = quantise("x", x_grp[k][:].rearrange("p e r t -> p (e r t)"), 2 * TOK, 2)

        def w1_tile(d):
            if d not in w1_grp:
                w1_grp[d] = work.tile([P, 2, 4, P, 4], BF16, name="w1_grp", align_bytes=64, bufs=4)
            return w1_grp[d]

        def w1_copy(d, experts, m=slice(0, P)):
            pairs = slice(m.start // RUN, m.stop // RUN)
            for i in range(experts.start, experts.stop):
                nc.scalar.copy(
                    out=w1_tile(d)[:, i].rearrange("p s (c r) t -> p c s t r", r=RUN)[:, pairs],
                    in_=w1_raw[d][:, i].rearrange("p t (c r s) -> p c s t r", r=RUN, s=4)[:, pairs],
                )

        def through_psum(d):
            return d >= G and d % G >= 2

        def w1_to_psum(d):
            src = w1_raw[d][:, 1].rearrange("p t (m s) -> p s m t", s=4)
            w1_ps[d] = []
            for a in range(2):
                bank = ps_t.tile([P, 2, 512], BF16, name="tp")
                for s in range(2):
                    nc.tensor.matmul(
                        out=bank[:, s, :], lhsT=ident_bf[:], rhs=src[:, 2 * a + s], start=True, stop=True
                    )
                w1_ps[d].append(bank)

        def w1_interleave(d):
            if d >= STEPS:
                return
            if through_psum(d):
                w1_copy(d, slice(0, 1))
                dst = w1_tile(d)[:, 1].rearrange("p s m t -> p (s m t)")
                for a, bank in enumerate(w1_ps[d]):
                    nc.scalar.copy(
                        out=dst[:, 1024 * a:1024 * (a + 1)].bitcast(F32),
                        in_=bank[:].rearrange("p s c -> p (s c)").bitcast(F32),
                    )
            else:
                w1_copy(d, slice(0, 2))
            load_w1(d + AHEAD)

        def w1_quantise(d):
            w1_cod[d] = quantise("w1", w1_grp[d][:].rearrange("p i s m t -> p (i s m t)"), 1024, G)

        def mm1(d):
            q, sc = w1_cod[d]
            xq, xs = x_cod[d // G]
            for i in range(2):
                ph = ps_h.tile([P, 4, TOK], F32, name="ph")
                tok = slice(i * TOK, (i + 1) * TOK)
                for s in range(4):
                    cols = slice((4 * i + s) * P, (4 * i + s + 1) * P)
                    nc.tensor.matmul_mx(
                        out=ph[:, s, :], lhsT=q[:, cols].bitcast(FP8X4), lhsT_scale=sc[:, cols],
                        rhs=xq[:, tok].bitcast(FP8X4), rhs_scale=xs[:, tok], start=True, stop=True,
                    )
                h_ps[d, i] = ph

        def h_bias(d):
            k, g = divmod(d, G)
            if k not in h_grp:
                h_grp[k] = work.tile([P, G, 2, TOK, 4], BF16, name="h_grp", align_bytes=64, bufs=1)
            for i in range(2):
                bias = b1_col[2 * k + i][:, g, 0:4].unsqueeze(1).unsqueeze(3)
                nc.vector.tensor_tensor(
                    out=h_grp[k][:, g, i].rearrange("p (c r) s -> p c s r", r=RUN),
                    in0=h_ps[d, i][:].rearrange("p s (c r) -> p c s r", r=RUN),
                    in1=bias.to_broadcast([P, TOK // RUN, 4, RUN]), op=ALU.add,
                )

        def h_relu(k):
            flat = h_grp[k][:].rearrange("p g i r s -> p (g i r s)")
            nc.vector.tensor_scalar_max(flat, flat, 0.0)

        def h_quantise(k):
            h_cod[k] = quantise("h", h_grp[k][:].rearrange("p g i r s -> p (g i r s)"), G * 2 * TOK, 2)

        def w2_widen(j, engine, cols=slice(0, COLS), slots=range(4)):
            if j not in w2_pl:
                w2_pl[j] = work.tile([P, 4, COLS], BF16, name="w2_pl", align_bytes=64, bufs=3)
            for s in slots:
                if j < LONG_ROWS:
                    src = w2_raw[j][:, cols.start // D, s, :].bitcast(FP8)
                else:
                    src = w2_raw[j][:, s].rearrange("p i n -> p (i n)").bitcast(FP8)
                dst = w2_pl[j][:, s, cols]
                if engine == "vector":
                    nc.vector.tensor_scalar(
                        out=dst, in0=src, scalar1=w2_scale(j % G, s), scalar2=None, op0=ALU.mult
                    )
                else:
                    nc.scalar.activation(out=dst, in_=src, func=ACT.Copy, scale=w2_scale(j % G, s))
            if cols.stop == COLS and slots.stop == 4:
                load_w2(j + AHEAD)

        def w2_tile(j):
            if j not in w2_grp:
                w2_grp[j] = work.tile([P, COLS, 4], BF16, name="w2_grp", align_bytes=64, bufs=4)
            return w2_grp[j]

        def w2_interleave(j, engine, cols=slice(0, COLS)):
            dst = w2_tile(j)[:, cols, :].rearrange("p (c r) s -> p c s r", r=RUN)
            src = w2_pl[j][:, :, cols].rearrange("p s (c r) -> p c s r", r=RUN)
            if engine == "vector":
                nc.vector.tensor_copy(out=dst, in_=src)
            elif engine == "scalar":
                nc.scalar.copy(out=dst, in_=src)
            else:
                nc.gpsimd.tensor_scalar(out=dst, in0=src, scalar1=1.0, scalar2=0.0, op0=ALU.mult, op1=ALU.add)

        def w2_through_psum(j, cols):
            src = w2_pl[j][:].rearrange("p s c -> p c s")
            bank = ps_t.tile([P, cols.stop - cols.start, 4], BF16, name="tp")
            for lo in range(cols.start, cols.stop, P):
                hi = min(lo + P, cols.stop)
                nc.tensor.matmul(
                    out=bank[:, lo - cols.start:hi - cols.start, :].rearrange("p c s -> p (c s)"),
                    lhsT=ident_bf[:], rhs=src[:, lo:hi, :], start=True, stop=True,
                )
            nc.scalar.copy(
                out=w2_tile(j)[:, cols, :].rearrange("p c s -> p (c s)").bitcast(F32),
                in_=bank[:].rearrange("p c s -> p (c s)").bitcast(F32),
            )

        def w2_quantise_part(j, cols):
            grp = w2_grp[j][:, cols, :].rearrange("p n s -> p (n s)")
            return quantise("w2", grp, cols.stop - cols.start, G)

        def w2_quantise(j):
            w2_cod[j] = w2_quantise_part(j, slice(0, COLS))

        def mm2_part(j, i, a, wq, ws, stop):
            k, g = divmod(j, G)
            hq, hs = h_cod[k]
            tok = slice((2 * g + i) * TOK, (2 * g + i + 1) * TOK)
            nc.tensor.matmul_mx(
                out=y_ps[2 * k + i][a][:], lhsT=hq[:, tok].bitcast(FP8X4), lhsT_scale=hs[:, tok],
                rhs=wq.bitcast(FP8X4), rhs_scale=ws, start=(g == 0), stop=stop,
            )

        def mm2(j):
            k, g = divmod(j, G)
            wq, ws = w2_cod[j]
            for i in range(2):
                e = 2 * k + i
                if g == 0 and e < E - 1:
                    y_ps[e] = [ps_y.tile([TOK, D], F32, name="py")]
                if g == 0 and e == E - 1:
                    y_ps[e] = [ps_y.tile([TOK, D // 2], F32, name="py"), ps_h.tile([TOK, D // 2], F32, name="ph")]
                width = D // len(y_ps[e])
                for a in range(len(y_ps[e])):
                    cols = slice(i * D + a * width, i * D + (a + 1) * width)
                    mm2_part(j, i, a, wq[:, cols], ws[:, cols], g == G - 1)

        def store(e, a=0, parts=1):
            width = D // parts
            cols = slice(a * width, (a + 1) * width)
            bank = y_ps[e][a][:] if len(y_ps[e]) > 1 else y_ps[e][0][:, cols]
            y = out_pool.tile([TOK, width], F32, name="y", align_bytes=64, bufs=4)
            nc.vector.scalar_tensor_tensor(
                out=y[:], in0=bank, scalar=gain[:], in1=b2_gain[e][:, cols],
                op0=ALU.mult, op1=ALU.add,
            )
            nc.sync.dma_start(out=out[e * TOK:(e + 1) * TOK, cols], in_=y[:])

        def window(k):
            d, j = G * k, 3 * k + 3
            w2_widen(j, "vector", slots=range(3, 4))
            w1_quantise(d + 2)
            if k == 0:
                w2_interleave(j, "gpsimd", slice(0, POOL_FIRST))
                w2_interleave(j, "scalar", slice(POOL_FIRST, COLS))
            else:
                w2_interleave(j, "gpsimd")
                w2_interleave(j + 1 if k == PAIRS - 1 else j - 1, "gpsimd", slice(0, POOL_EXTRA))
            if k + 1 < PAIRS:
                x_copy(k + 1)
            h_bias(d)
            mm1(d + 2)
            h_bias(d + 1)
            mm1(d + 3)
            if k > 0:
                store(2 * k - 2)
                store(2 * k - 1)
            h_bias(d + 2)
            h_bias(d + 3)
            load_b2(k)

        def h_finish(k, j):
            w2_widen(j, "vector", slots=range(1))
            h_relu(k)
            w2_widen(j, "vector", slots=range(1, 4))
            h_quantise(k)

        first, second = slice(0, D), slice(D, COLS)
        w2_widen(0, "vector", first)
        w2_widen(0, "vector", second)
        w1_copy(0, slice(0, 1), slice(0, 64))
        w1_copy(0, slice(0, 1), slice(64, P))
        w1_copy(0, slice(1, 2))
        load_w1(AHEAD + 1)
        w2_interleave(0, "vector", first)
        w2_interleave(0, "vector", second)
        w2_widen(1, "vector", first)
        w2_widen(1, "vector", second)
        w2_quantise(0)
        w1_quantise(0)
        w1_copy(1, slice(0, 1))
        w1_copy(1, slice(1, 2))
        w2_interleave(1, "vector")
        w2_widen(2, "vector")
        w2_quantise(1)
        w1_quantise(1)
        w1_copy(2, slice(0, 1))
        w1_copy(2, slice(1, 2))
        load_w1(2 + AHEAD)
        x_turn(0)
        x_copy(0)
        w2_interleave(2, "vector", slice(0, V_COLS_HEAD))
        park_b2()
        x_quantise(0)
        mm1(0)
        mm1(1)
        w1_interleave(3)
        w2_interleave(2, "scalar", slice(V_COLS_HEAD, COLS))
        load_b1(1)
        w2_widen(3, "vector", slots=range(3))
        w1_quantise(3)
        x_turn(1)
        w1_interleave(4)
        window(0)

        for k in range(1, PAIRS):
            d, j = G * k, 3 * k
            last = k == PAIRS - 1
            w1_interleave(d + 1)
            w1_to_psum(d + 2)
            h_finish(k - 1, j + 1)
            w2_quantise(j - 1)
            w1_interleave(d + 2)
            w1_to_psum(d + 3)
            if not last:
                load_x(k + 1)
                load_b1(k + 1)
            for ready in range(d - G, j):
                mm2(ready)
            w2_widen(j + 2, "vector")
            w2_quantise(j)
            mm2(j)
            w1_quantise(d)
            x_quantise(k)
            w1_quantise(d + 1)
            mm1(d)
            mm1(d + 1)
            w2_interleave(j + 1, "scalar")
            w1_interleave(d + 3)
            if last:
                w2_interleave(j + 2, "vector", slice(0, V_COLS))
                w2_interleave(j + 2, "scalar", slice(V_COLS, COLS - PE_COLS))
                w2_through_psum(j + 2, slice(COLS - PE_COLS, COLS))
            else:
                w2_interleave(j + 2, "vector", slice(POOL_EXTRA, V_COLS))
                w2_interleave(j + 2, "scalar", slice(V_COLS, COLS))
            w2_quantise(j + 1)
            if j + 1 < d:
                mm2(j + 1)
            if not last:
                x_turn(k + 1)
            w2_widen(j + 3, "vector", slots=range(3))
            w1_quantise(d + 3)
            w1_interleave(d + 4)
            if last:
                w2_quantise(j + 2)
                mm2(j + 2)
                w2_widen(j + 4, "scalar")
            window(k)

        j = STEPS - G
        half = D // 2
        halves = [slice(D + half * a, D + half * (a + 1)) for a in range(2)]
        w2_widen(j + 2, "scalar")
        h_finish(PAIRS - 1, j + 3)
        w2_quantise(j)
        mm2(j)
        w2_interleave(j + 1, "scalar", slice(POOL_EXTRA, COLS))
        w2_quantise(j + 1)
        mm2(j + 1)
        w2_interleave(j + 2, "vector", slice(0, V_COLS_TAIL))
        w2_interleave(j + 3, "vector", first)
        w2_interleave(j + 2, "scalar", slice(V_COLS_TAIL, COLS))
        for cols in halves:
            w2_interleave(j + 3, "scalar", cols)
        for step in (j + 2, j + 3):
            wq, ws = w2_quantise_part(step, first)
            mm2_part(step, 0, 0, wq[:], ws[:], step == j + 3)
        wq, ws = w2_quantise_part(j + 2, second)
        for a in range(2):
            mm2_part(j + 2, 1, a, wq[:, half * a:half * (a + 1)], ws[:, half * a:half * (a + 1)], False)
        for a in range(2):
            wq, ws = w2_quantise_part(j + 3, halves[a])
            mm2_part(j + 3, 1, a, wq[:], ws[:], True)
        for e in (E - 2, E - 1):
            for a in range(2):
                store(e, a, 2)
